import numpy as np
import ml_dtypes

BF16 = ml_dtypes.bfloat16


def bf(x):
    return np.asarray(x, np.float32).astype(BF16)


def f32(x):
    return np.asarray(x, np.float32)


def f64(x):
    return np.asarray(x).astype(np.float64)


def striped(idx):
    return np.tile(idx.reshape(-1, 16).T, (8, 1))


C, S, DIN, DOUT, F, N, DEG, H = 256, 256, 512, 512, 256, 8192, 32, 128
ALPHA = 0.2
NEG_BIG = -9e15


def setup_inputs():
    h = f32(np.random.standard_normal((DIN, S)))
    W = bf(np.random.standard_normal((DIN, DOUT)) / np.sqrt(DIN))
    a1 = bf(np.concatenate([np.random.standard_normal((DOUT, C)) / np.sqrt(DOUT), np.random.standard_normal((DOUT, C)) / np.sqrt(DOUT), np.random.standard_normal((F, C)) / np.sqrt(F)], axis=0))
    ef = bf(np.random.standard_normal((F, N)))
    a3 = bf(np.random.standard_normal((N, S)) * (2.0 / np.sqrt(3.0 * N)))
    idx = np.concatenate([np.random.permutation(S)[:H] for _ in range(N // H)])
    return {"h": h, "W": W, "a1": a1, "ef": ef, "a3": a3, "offs": striped(idx)}


def reference(h, W, a1, ef, a3, offs):
    idx = offs[:16].T.reshape(-1)
    wh = f64(W).T @ f64(h)
    a = f64(a1)
    P = a[:DOUT].T @ wh
    Q = a[DOUT:DOUT + DOUT].T @ wh
    R = a[DOUT + DOUT:].T @ f64(ef)
    nee = P[:, idx] + (np.repeat(Q, DEG, axis=1) + R)
    e = f64(a3).T @ nee.T
    e = np.maximum(e, ALPHA * e)
    e = np.where(np.eye(S, dtype=bool), NEG_BIG, e)
    e = e - e.max(axis=1, keepdims=True)
    w = np.exp(e)
    att = w / w.sum(axis=1, keepdims=True)
    return wh @ att.T

@@ -1,0 +1,204 @@
+from contextlib import ExitStack
+
+import concourse.mybir as mybir
+from concourse.masks import make_identity
+
+F32 = mybir.dt.float32
+BF16 = mybir.dt.bfloat16
+U16 = mybir.dt.uint16
+ADD = mybir.AluOpType.add
+MAX = mybir.AluOpType.max
+EXP = mybir.ActivationFunctionType.Exp
+FREE_AXIS = mybir.AxisListType.X
+
+P = 128
+D_IN, D_OUT, D_EDGE = 512, 512, 256
+NODES, EDGES, DEGREE = 256, 8192, 32
+ALPHA = 0.2
+NEG_BIG = -9e15
+
+K_IN, K_OUT, K_EDGE = D_IN // P, D_OUT // P, D_EDGE // P
+BLOCKS = NODES // P
+CHUNK = 512
+PIECE = 256
+CHUNKS = EDGES // CHUNK
+PIECES = CHUNK // PIECE
+EF_COLS = 2048
+A3_BLOCKS = 8
+
+FLOPS = 2 * (D_IN * D_OUT * NODES + 2 * D_OUT * NODES * NODES + D_EDGE * NODES * EDGES
+             + EDGES * NODES * NODES + NODES * NODES * D_OUT)
+
+
+def tile_graphattentionlayer_b_kernel(tc, h, W, a1, ef, a3, offs, out):
+    nc = tc.nc
+    with ExitStack() as pools:
+        held = pools.enter_context(tc.tile_pool(name="held", bufs=1))
+        sums = pools.enter_context(tc.tile_pool(name="sums", bufs=4))
+        picked = pools.enter_context(tc.tile_pool(name="picked", bufs=8))
+        flipped = pools.enter_context(tc.tile_pool(name="flipped", bufs=4))
+        tail = pools.enter_context(tc.tile_pool(name="tail", bufs=2))
+        banks = pools.enter_context(tc.psum_pool(name="banks", bufs=4))
+        flips = pools.enter_context(tc.psum_pool(name="flips", bufs=2))
+        scores = pools.enter_context(tc.psum_pool(name="scores", bufs=1))
+
+        h_f32 = held.tile([P, K_IN, NODES], F32, name="h_f32")
+        nc.sync.dma_start(h_f32[:], h.rearrange("(k p) s -> p k s", p=P))
+        w_sb = held.tile([P, K_IN, D_OUT], BF16, name="w_sb")
+        nc.scalar.dma_start(w_sb[:], W.rearrange("(k p) d -> p k d", p=P))
+        a1_sb = held.tile([P, 2 * K_OUT + K_EDGE, NODES], BF16, name="a1_sb")
+        nc.scalar.dma_start(a1_sb[:], a1.rearrange("(k p) c -> p k c", p=P))
+        offsets = held.tile([P, EDGES // 16], U16, name="offsets")
+        nc.sync.dma_start(offsets[:], offs)
+        ef_sb = [[held.tile([P, EF_COLS], BF16, name=f"ef_{k}_{g}") for g in range(EDGES // EF_COLS)]
+                 for k in range(K_EDGE)]
+        a3_sb = [held.tile([P, A3_BLOCKS, NODES], BF16, name=f"a3_{g}")
+                 for g in range(EDGES // (A3_BLOCKS * P))]
+        a3_per_ef = EF_COLS // (A3_BLOCKS * P)
+        for g in range(EDGES // EF_COLS):
+            for k in range(K_EDGE):
+                nc.sync.dma_start(ef_sb[k][g][:], ef[k * P:(k + 1) * P, g * EF_COLS:(g + 1) * EF_COLS])
+            for g3 in range(g * a3_per_ef, (g + 1) * a3_per_ef):
+                rows = a3[g3 * A3_BLOCKS * P:(g3 + 1) * A3_BLOCKS * P, :]
+                nc.sync.dma_start(a3_sb[g3][:], rows.rearrange("(b p) s -> p b s", p=P))
+
+        identity = held.tile([P, P], F32, name="identity")
+        make_identity(nc, identity[:])
+        self_mask = held.tile([P, P], F32, name="self_mask")
+        nc.vector.tensor_scalar_mul(self_mask[:], identity[:], NEG_BIG)
+
+        h_bf = held.tile([P, K_IN, NODES], BF16, name="h_bf")
+        nc.vector.tensor_copy(h_bf[:], h_f32[:])
+        wh_bf = held.tile([P, K_OUT, NODES], BF16, name="wh_bf")
+        for pair in range(K_OUT // 2):
+            wh_ps = banks.tile([P, 2, NODES], F32, name="bank")
+            for half in range(2):
+                d = 2 * pair + half
+                for k in range(K_IN):
+                    nc.tensor.matmul(wh_ps[:, half, :], w_sb[:, k, d * P:(d + 1) * P], h_bf[:, k, :],
+                                     start=(k == 0), stop=(k == K_IN - 1))
+            nc.vector.tensor_copy(wh_bf[:, 2 * pair:2 * pair + 2, :], wh_ps[:])
+
+        p_sb = [held.tile([P, NODES], F32, name=f"p_{c}") for c in range(BLOCKS)]
+        q_sb = [held.tile([P, NODES], F32, name=f"q_{c}") for c in range(BLOCKS)]
+        for c in range(BLOCKS):
+            pq_ps = banks.tile([P, 2, NODES], F32, name="bank")
+            for role in range(2):
+                for k in range(K_OUT):
+                    nc.tensor.matmul(pq_ps[:, role, :], a1_sb[:, role * K_OUT + k, c * P:(c + 1) * P],
+                                     wh_bf[:, k, :], start=(k == 0), stop=(k == K_OUT - 1))
+            nc.vector.tensor_copy(p_sb[c][:], pq_ps[:, 0, :])
+            nc.vector.tensor_copy(q_sb[c][:], pq_ps[:, 1, :])
+
+        e_ps = [scores.tile([P, NODES], F32, name=f"e_{b}") for b in range(BLOCKS)]
+
+        def project_edges(t):
+            r_ps = []
+            for c in range(BLOCKS):
+                bank = banks.tile([P, CHUNK], F32, name="bank")
+                first = (t * CHUNK) % EF_COLS
+                for k in range(K_EDGE):
+                    nc.tensor.matmul(bank[:], a1_sb[:, 2 * K_OUT + k, c * P:(c + 1) * P],
+                                     ef_sb[k][t * CHUNK // EF_COLS][:, first:first + CHUNK],
+                                     start=(k == 0), stop=(k == K_EDGE - 1))
+                r_ps.append(bank)
+            return r_ps
+
+        def look_up(t, r_ps):
+            per_chunk = CHUNK // DEGREE
+            qr_sb = []
+            for c in range(BLOCKS):
+                qr = sums.tile([P, CHUNK], F32, name="qr")
+                nc.vector.tensor_tensor(
+                    qr[:].rearrange("p (s e) -> p s e", e=DEGREE),
+                    r_ps[c][:].rearrange("p (s e) -> p s e", e=DEGREE),
+                    q_sb[c][:, t * per_chunk:(t + 1) * per_chunk].unsqueeze(2).to_broadcast([P, per_chunk, DEGREE]),
+                    ADD)
+                qr_sb.append(qr)
+            nee_sb = []
+            for piece in range(PIECES):
+                column = (t * CHUNK + piece * PIECE) // 16
+                both = []
+                for c in range(BLOCKS):
+                    nee = picked.tile([P, PIECE], F32, name="nee")
+                    nc.vector.tensor_tensor(nee[:], p_sb[c][:].indirect(offsets[:, column:column + PIECE // 16]),
+                                            qr_sb[c][:, piece * PIECE:(piece + 1) * PIECE], ADD)
+                    both.append(nee)
+                nee_sb.append(both)
+            return nee_sb
+
+        def flip(nee_sb):
+            nee_t = []
+            for piece in range(PIECES):
+                flip_ps = flips.tile([P, PIECE // P, NODES], F32, name="flip")
+                for b in range(PIECE // P):
+                    for c in range(BLOCKS):
+                        nc.tensor.transpose(flip_ps[:, b, c * P:(c + 1) * P], nee_sb[piece][c][:, b * P:(b + 1) * P],
+                                            identity[:])
+                turned = flipped.tile([P, PIECE // P, NODES], BF16, name="turned")
+                nc.scalar.copy(turned[:], flip_ps[:])
+                nee_t.append(turned)
+            return nee_t
+
+        def mix(t, nee_t):
+            for piece in range(PIECES):
+                for b in range(PIECE // P):
+                    j = (t * CHUNK + piece * PIECE) // P + b
+                    for pb in range(BLOCKS):
+                        nc.tensor.matmul(e_ps[pb][:], a3_sb[j // A3_BLOCKS][:, j % A3_BLOCKS, pb * P:(pb + 1) * P],
+                                         nee_t[piece][:, b, :], start=(j == 0), stop=(j == EDGES // P - 1))
+
+        r_next = project_edges(0)
+        nee_t_last = None
+        for t in range(CHUNKS):
+            r_now = r_next
+            if t + 1 < CHUNKS:
+                r_next = project_edges(t + 1)
+            nee_sb = look_up(t, r_now)
+            if t > 0:
+                mix(t - 1, nee_t_last)
+            nee_t_last = flip(nee_sb)
+
+        wh_t_bf = held.tile([P, BLOCKS, D_OUT], BF16, name="wh_t_bf")
+        for s in range(BLOCKS):
+            wh_t_ps = banks.tile([P, D_OUT], F32, name="bank")
+            for k in range(K_IN):
+                nc.tensor.matmul(wh_t_ps[:], h_bf[:, k, s * P:(s + 1) * P], w_sb[:, k, :],
+                                 start=(k == 0), stop=(k == K_IN - 1))
+            nc.scalar.copy(wh_t_bf[:, s, :], wh_t_ps[:])
+
+        mix(CHUNKS - 1, nee_t_last)
+
+        att_t_ps = flips.tile([P, BLOCKS, NODES], F32, name="flip")
+        for pb in range(BLOCKS):
+            scaled = tail.tile([P, NODES], F32, name="scaled")
+            nc.vector.tensor_scalar_mul(scaled[:], e_ps[pb][:], ALPHA)
+            score = tail.tile([P, NODES], F32, name="score")
+            nc.vector.tensor_tensor(score[:], e_ps[pb][:], scaled[:], MAX)
+            own = score[:, pb * P:(pb + 1) * P]
+            nc.vector.tensor_tensor(own, own, self_mask[:], ADD)
+            neg_top = tail.tile([P, 1], F32, name="neg_top")
+            nc.vector.reduce_max(neg_top[:], score[:], FREE_AXIS, negate=True)
+            weight = tail.tile([P, NODES], F32, name="weight")
+            total = tail.tile([P, 1], F32, name="total")
+            nc.scalar.activation(weight[:], score[:], EXP, bias=neg_top[:], accum_out=total[:])
+            inverse = tail.tile([P, 1], F32, name="inverse")
+            nc.vector.reciprocal(inverse[:], total[:])
+            att = tail.tile([P, NODES], F32, name="att")
+            nc.vector.tensor_scalar_mul(att[:], weight[:], inverse[:])
+            for c in range(BLOCKS):
+                nc.tensor.transpose(att_t_ps[:, c, pb * P:(pb + 1) * P], att[:, c * P:(c + 1) * P], identity[:])
+        att_t_bf = held.tile([P, BLOCKS, NODES], BF16, name="att_t_bf")
+        nc.vector.tensor_copy(att_t_bf[:], att_t_ps[:])
+
+        out_blocks = out.rearrange("(k p) s -> p k s", p=P)
+        for pair in range(K_OUT // 2):
+            out_ps = banks.tile([P, 2, NODES], F32, name="bank")
+            for half in range(2):
+                d = 2 * pair + half
+                for c in range(BLOCKS):
+                    nc.tensor.matmul(out_ps[:, half, :], wh_t_bf[:, c, d * P:(d + 1) * P], att_t_bf[:, c, :],
+                                     start=(c == 0), stop=(c == BLOCKS - 1))
+            out_sb = tail.tile([P, 2, NODES], F32, name="out_sb")
+            nc.vector.tensor_copy(out_sb[:], out_ps[:])
+            nc.sync.dma_start(out_blocks[:, 2 * pair:2 * pair + 2, :], out_sb[:])

@@ -9,6 +9,7 @@ U16 = mybir.dt.uint16
 ADD = mybir.AluOpType.add
 MAX = mybir.AluOpType.max
 EXP = mybir.ActivationFunctionType.Exp
+IDENTITY = mybir.ActivationFunctionType.Identity
 FREE_AXIS = mybir.AxisListType.X
 
 P = 128
@@ -34,7 +35,7 @@ def tile_graphattentionlayer_b_kernel(tc, h, W, a1, ef, a3, offs, out):
     nc = tc.nc
     with ExitStack() as pools:
         held = pools.enter_context(tc.tile_pool(name="held", bufs=1))
-        sums = pools.enter_context(tc.tile_pool(name="sums", bufs=4))
+        sums = pools.enter_context(tc.tile_pool(name="sums", bufs=6))
         picked = pools.enter_context(tc.tile_pool(name="picked", bufs=8))
         flipped = pools.enter_context(tc.tile_pool(name="flipped", bufs=4))
         tail = pools.enter_context(tc.tile_pool(name="tail", bufs=2))
@@ -104,17 +105,22 @@ def tile_graphattentionlayer_b_kernel(tc, h, W, a1, ef, a3, offs, out):
                 r_ps.append(bank)
             return r_ps
 
-        def look_up(t, r_ps):
+        def add_targets(t, r_ps):
             per_chunk = CHUNK // DEGREE
-            qr_sb = []
-            for c in range(BLOCKS):
-                qr = sums.tile([P, CHUNK], F32, name="qr")
-                nc.vector.tensor_tensor(
-                    qr[:].rearrange("p (s e) -> p s e", e=DEGREE),
-                    r_ps[c][:].rearrange("p (s e) -> p s e", e=DEGREE),
-                    q_sb[c][:, t * per_chunk:(t + 1) * per_chunk].unsqueeze(2).to_broadcast([P, per_chunk, DEGREE]),
-                    ADD)
-                qr_sb.append(qr)
+            by_vector = sums.tile([P, CHUNK], F32, name="qr")
+            nc.vector.tensor_tensor(
+                by_vector[:].rearrange("p (s e) -> p s e", e=DEGREE),
+                r_ps[0][:].rearrange("p (s e) -> p s e", e=DEGREE),
+                q_sb[0][:, t * per_chunk:(t + 1) * per_chunk].unsqueeze(2).to_broadcast([P, per_chunk, DEGREE]),
+                ADD)
+            by_scalar = sums.tile([P, CHUNK], F32, name="qr")
+            for s in range(per_chunk):
+                node = t * per_chunk + s
+                nc.scalar.activation(by_scalar[:, s * DEGREE:(s + 1) * DEGREE], r_ps[1][:, s * DEGREE:(s + 1) * DEGREE],
+                                     IDENTITY, bias=q_sb[1][:, node:node + 1])
+            return [by_vector, by_scalar]
+
+        def look_up(t, qr_sb):
             nee_sb = []
             for piece in range(PIECES):
                 column = (t * CHUNK + piece * PIECE) // 16
@@ -148,13 +154,16 @@ def tile_graphattentionlayer_b_kernel(tc, h, W, a1, ef, a3, offs, out):
                         nc.tensor.matmul(e_ps[pb][:], a3_sb[j // A3_BLOCKS][:, j % A3_BLOCKS, pb * P:(pb + 1) * P],
                                          nee_t[piece][:, b, :], start=(j == 0), stop=(j == EDGES // P - 1))
 
-        r_next = project_edges(0)
+        qr_next = add_targets(0, project_edges(0))
+        r_next = project_edges(1)
         nee_t_last = None
         for t in range(CHUNKS):
-            r_now = r_next
+            qr_now = qr_next
             if t + 1 < CHUNKS:
-                r_next = project_edges(t + 1)
-            nee_sb = look_up(t, r_now)
+                qr_next = add_targets(t + 1, r_next)
+            if t + 2 < CHUNKS:
+                r_next = project_edges(t + 2)
+            nee_sb = look_up(t, qr_now)
             if t > 0:
                 mix(t - 1, nee_t_last)
             nee_t_last = flip(nee_sb)

@@ -26,6 +26,7 @@ CHUNKS = EDGES // CHUNK
 PIECES = CHUNK // PIECE
 EF_COLS = 2048
 A3_BLOCKS = 8
+WARM_UP = 7
 
 FLOPS = 2 * (D_IN * D_OUT * NODES + 2 * D_OUT * NODES * NODES + D_EDGE * NODES * EDGES
              + EDGES * NODES * NODES + NODES * NODES * D_OUT)
@@ -50,7 +51,6 @@ def tile_graphattentionlayer_b_kernel(tc, h, W, a1, ef, a3, offs, out):
         a1_sb = held.tile([P, 2 * K_OUT + K_EDGE, NODES], BF16, name="a1_sb")
         nc.scalar.dma_start(a1_sb[:], a1.rearrange("(k p) c -> p k c", p=P))
         offsets = held.tile([P, EDGES // 16], U16, name="offsets")
-        nc.sync.dma_start(offsets[:], offs)
         ef_sb = [[held.tile([P, EF_COLS], BF16, name=f"ef_{k}_{g}") for g in range(EDGES // EF_COLS)]
                  for k in range(K_EDGE)]
         a3_sb = [held.tile([P, A3_BLOCKS, NODES], BF16, name=f"a3_{g}")
@@ -59,6 +59,8 @@ def tile_graphattentionlayer_b_kernel(tc, h, W, a1, ef, a3, offs, out):
         for g in range(EDGES // EF_COLS):
             for k in range(K_EDGE):
                 nc.sync.dma_start(ef_sb[k][g][:], ef[k * P:(k + 1) * P, g * EF_COLS:(g + 1) * EF_COLS])
+            if g == 0:
+                nc.sync.dma_start(offsets[:], offs)
             for g3 in range(g * a3_per_ef, (g + 1) * a3_per_ef):
                 rows = a3[g3 * A3_BLOCKS * P:(g3 + 1) * A3_BLOCKS * P, :]
                 nc.sync.dma_start(a3_sb[g3][:], rows.rearrange("(b p) s -> p b s", p=P))
@@ -67,6 +69,14 @@ def tile_graphattentionlayer_b_kernel(tc, h, W, a1, ef, a3, offs, out):
         make_identity(nc, identity[:])
         self_mask = held.tile([P, P], F32, name="self_mask")
         nc.vector.tensor_scalar_mul(self_mask[:], identity[:], NEG_BIG)
+
+        zeros = held.tile([P, CHUNK], BF16, name="zeros")
+        nc.vector.memset(zeros[:], 0.0)
+        idle_ps = flips.tile([P, CHUNK], F32, name="flip")
+        for i in range(WARM_UP):
+            nc.tensor.matmul(idle_ps[:], zeros[:, 0:P], zeros[:], start=True, stop=True)
+        one = held.tile([P, 1], F32, name="one")
+        nc.scalar.activation(one[:], zeros[:, 0:1], EXP)
 
         h_bf = held.tile([P, K_IN, NODES], BF16, name="h_bf")
         nc.vector.tensor_copy(h_bf[:], h_f32[:])
@@ -78,18 +88,24 @@ def tile_graphattentionlayer_b_kernel(tc, h, W, a1, ef, a3, offs, out):
                 for k in range(K_IN):
                     nc.tensor.matmul(wh_ps[:, half, :], w_sb[:, k, d * P:(d + 1) * P], h_bf[:, k, :],
                                      start=(k == 0), stop=(k == K_IN - 1))
-            nc.vector.tensor_copy(wh_bf[:, 2 * pair:2 * pair + 2, :], wh_ps[:])
+            if pair == 0:
+                nc.vector.tensor_copy(wh_bf[:, 0:2, :], wh_ps[:])
+            else:
+                nc.scalar.copy(wh_bf[:, 2:4, :], wh_ps[:])
 
         p_sb = [held.tile([P, NODES], F32, name=f"p_{c}") for c in range(BLOCKS)]
         q_sb = [held.tile([P, NODES], F32, name=f"q_{c}") for c in range(BLOCKS)]
-        for c in range(BLOCKS):
-            pq_ps = banks.tile([P, 2, NODES], F32, name="bank")
-            for role in range(2):
+        for role, kept in enumerate((p_sb, q_sb)):
+            role_ps = banks.tile([P, BLOCKS, NODES], F32, name="bank")
+            for c in range(BLOCKS):
                 for k in range(K_OUT):
-                    nc.tensor.matmul(pq_ps[:, role, :], a1_sb[:, role * K_OUT + k, c * P:(c + 1) * P],
+                    nc.tensor.matmul(role_ps[:, c, :], a1_sb[:, role * K_OUT + k, c * P:(c + 1) * P],
                                      wh_bf[:, k, :], start=(k == 0), stop=(k == K_OUT - 1))
-            nc.vector.tensor_copy(p_sb[c][:], pq_ps[:, 0, :])
-            nc.vector.tensor_copy(q_sb[c][:], pq_ps[:, 1, :])
+            for c in range(BLOCKS):
+                if role == 0:
+                    nc.vector.tensor_copy(kept[c][:], role_ps[:, c, :])
+                else:
+                    nc.scalar.copy(kept[c][:], role_ps[:, c, :])
 
         e_ps = [scores.tile([P, NODES], F32, name=f"e_{b}") for b in range(BLOCKS)]
 
@@ -156,6 +172,15 @@ def tile_graphattentionlayer_b_kernel(tc, h, W, a1, ef, a3, offs, out):
 
         qr_next = add_targets(0, project_edges(0))
         r_next = project_edges(1)
+
+        wh_t_bf = held.tile([P, BLOCKS, D_OUT], BF16, name="wh_t_bf")
+        for s in range(BLOCKS):
+            wh_t_ps = flips.tile([P, D_OUT], F32, name="flip")
+            for k in range(K_IN):
+                nc.tensor.matmul(wh_t_ps[:], h_bf[:, k, s * P:(s + 1) * P], w_sb[:, k, :],
+                                 start=(k == 0), stop=(k == K_IN - 1))
+            nc.scalar.copy(wh_t_bf[:, s, :], wh_t_ps[:])
+
         nee_t_last = None
         for t in range(CHUNKS):
             qr_now = qr_next
@@ -167,21 +192,12 @@ def tile_graphattentionlayer_b_kernel(tc, h, W, a1, ef, a3, offs, out):
             if t > 0:
                 mix(t - 1, nee_t_last)
             nee_t_last = flip(nee_sb)
-
-        wh_t_bf = held.tile([P, BLOCKS, D_OUT], BF16, name="wh_t_bf")
-        for s in range(BLOCKS):
-            wh_t_ps = banks.tile([P, D_OUT], F32, name="bank")
-            for k in range(K_IN):
-                nc.tensor.matmul(wh_t_ps[:], h_bf[:, k, s * P:(s + 1) * P], w_sb[:, k, :],
-                                 start=(k == 0), stop=(k == K_IN - 1))
-            nc.scalar.copy(wh_t_bf[:, s, :], wh_t_ps[:])
-
         mix(CHUNKS - 1, nee_t_last)
 
-        att_t_ps = flips.tile([P, BLOCKS, NODES], F32, name="flip")
+        att_t_ps = [flips.tile([P, NODES], F32, name="flip") for c in range(BLOCKS)]
         for pb in range(BLOCKS):
             scaled = tail.tile([P, NODES], F32, name="scaled")
-            nc.vector.tensor_scalar_mul(scaled[:], e_ps[pb][:], ALPHA)
+            nc.scalar.mul(scaled[:], e_ps[pb][:], ALPHA)
             score = tail.tile([P, NODES], F32, name="score")
             nc.vector.tensor_tensor(score[:], e_ps[pb][:], scaled[:], MAX)
             own = score[:, pb * P:(pb + 1) * P]
@@ -196,9 +212,10 @@ def tile_graphattentionlayer_b_kernel(tc, h, W, a1, ef, a3, offs, out):
             att = tail.tile([P, NODES], F32, name="att")
             nc.vector.tensor_scalar_mul(att[:], weight[:], inverse[:])
             for c in range(BLOCKS):
-                nc.tensor.transpose(att_t_ps[:, c, pb * P:(pb + 1) * P], att[:, c * P:(c + 1) * P], identity[:])
+                nc.tensor.transpose(att_t_ps[c][:, pb * P:(pb + 1) * P], att[:, c * P:(c + 1) * P], identity[:])
         att_t_bf = held.tile([P, BLOCKS, NODES], BF16, name="att_t_bf")
-        nc.vector.tensor_copy(att_t_bf[:], att_t_ps[:])
+        nc.vector.tensor_copy(att_t_bf[:, 0, :], att_t_ps[0][:])
+        nc.scalar.copy(att_t_bf[:, 1, :], att_t_ps[1][:])
 
         out_blocks = out.rearrange("(k p) s -> p k s", p=P)
         for pair in range(K_OUT // 2):
@@ -209,5 +226,9 @@ def tile_graphattentionlayer_b_kernel(tc, h, W, a1, ef, a3, offs, out):
                     nc.tensor.matmul(out_ps[:, half, :], wh_t_bf[:, c, d * P:(d + 1) * P], att_t_bf[:, c, :],
                                      start=(c == 0), stop=(c == BLOCKS - 1))
             out_sb = tail.tile([P, 2, NODES], F32, name="out_sb")
-            nc.vector.tensor_copy(out_sb[:], out_ps[:])
-            nc.sync.dma_start(out_blocks[:, 2 * pair:2 * pair + 2, :], out_sb[:])
+            if pair == 0:
+                nc.vector.tensor_copy(out_sb[:], out_ps[:])
+                nc.sync.dma_start(out_blocks[:, 0:2, :], out_sb[:])
+            else:
+                nc.scalar.copy(out_sb[:], out_ps[:])
+                nc.scalar.dma_start(out_blocks[:, 2:4, :], out_sb[:])

@@ -24,9 +24,8 @@ CHUNK = 512
 PIECE = 256
 CHUNKS = EDGES // CHUNK
 PIECES = CHUNK // PIECE
-EF_COLS = 2048
-A3_BLOCKS = 8
-WARM_UP = 7
+GROUP = 1024
+WARM_UP = 3
 
 FLOPS = 2 * (D_IN * D_OUT * NODES + 2 * D_OUT * NODES * NODES + D_EDGE * NODES * EDGES
              + EDGES * NODES * NODES + NODES * NODES * D_OUT)
@@ -44,31 +43,25 @@ def tile_graphattentionlayer_b_kernel(tc, h, W, a1, ef, a3, offs, out):
         flips = pools.enter_context(tc.psum_pool(name="flips", bufs=2))
         scores = pools.enter_context(tc.psum_pool(name="scores", bufs=1))
 
-        h_f32 = held.tile([P, K_IN, NODES], F32, name="h_f32")
-        nc.sync.dma_start(h_f32[:], h.rearrange("(k p) s -> p k s", p=P))
-        w_sb = held.tile([P, K_IN, D_OUT], BF16, name="w_sb")
-        nc.scalar.dma_start(w_sb[:], W.rearrange("(k p) d -> p k d", p=P))
-        a1_sb = held.tile([P, 2 * K_OUT + K_EDGE, NODES], BF16, name="a1_sb")
-        nc.scalar.dma_start(a1_sb[:], a1.rearrange("(k p) c -> p k c", p=P))
+        h_f32 = [held.tile([P, NODES], F32, name=f"h_f32_{k}") for k in range(K_IN)]
+        w_sb = [held.tile([P, D_OUT], BF16, name=f"w_{k}") for k in range(K_IN)]
+        for k in range(K_IN):
+            nc.sync.dma_start(h_f32[k][:], h[k * P:(k + 1) * P, :])
+            nc.scalar.dma_start(w_sb[k][:], W[k * P:(k + 1) * P, :])
+        a1_nodes = held.tile([P, 2 * K_OUT, NODES], BF16, name="a1_nodes")
+        nc.scalar.dma_start(a1_nodes[:], a1[0:2 * D_OUT, :].rearrange("(k p) c -> p k c", p=P))
+        a1_edges = held.tile([P, K_EDGE, NODES], BF16, name="a1_edges")
+        nc.scalar.dma_start(a1_edges[:], a1[2 * D_OUT:2 * D_OUT + D_EDGE, :].rearrange("(k p) c -> p k c", p=P))
         offsets = held.tile([P, EDGES // 16], U16, name="offsets")
-        ef_sb = [[held.tile([P, EF_COLS], BF16, name=f"ef_{k}_{g}") for g in range(EDGES // EF_COLS)]
+        ef_sb = [[held.tile([P, GROUP], BF16, name=f"ef_{k}_{g}") for g in range(EDGES // GROUP)]
                  for k in range(K_EDGE)]
-        a3_sb = [held.tile([P, A3_BLOCKS, NODES], BF16, name=f"a3_{g}")
-                 for g in range(EDGES // (A3_BLOCKS * P))]
-        a3_per_ef = EF_COLS // (A3_BLOCKS * P)
-        for g in range(EDGES // EF_COLS):
+        a3_sb = [held.tile([P, GROUP // P, NODES], BF16, name=f"a3_{g}") for g in range(EDGES // GROUP)]
+        for g in range(EDGES // GROUP):
             for k in range(K_EDGE):
-                nc.sync.dma_start(ef_sb[k][g][:], ef[k * P:(k + 1) * P, g * EF_COLS:(g + 1) * EF_COLS])
+                nc.sync.dma_start(ef_sb[k][g][:], ef[k * P:(k + 1) * P, g * GROUP:(g + 1) * GROUP])
             if g == 0:
                 nc.sync.dma_start(offsets[:], offs)
-            for g3 in range(g * a3_per_ef, (g + 1) * a3_per_ef):
-                rows = a3[g3 * A3_BLOCKS * P:(g3 + 1) * A3_BLOCKS * P, :]
-                nc.sync.dma_start(a3_sb[g3][:], rows.rearrange("(b p) s -> p b s", p=P))
-
-        identity = held.tile([P, P], F32, name="identity")
-        make_identity(nc, identity[:])
-        self_mask = held.tile([P, P], F32, name="self_mask")
-        nc.vector.tensor_scalar_mul(self_mask[:], identity[:], NEG_BIG)
+            nc.sync.dma_start(a3_sb[g][:], a3[g * GROUP:(g + 1) * GROUP, :].rearrange("(b p) s -> p b s", p=P))
 
         zeros = held.tile([P, CHUNK], BF16, name="zeros")
         nc.vector.memset(zeros[:], 0.0)
@@ -78,34 +71,38 @@ def tile_graphattentionlayer_b_kernel(tc, h, W, a1, ef, a3, offs, out):
         one = held.tile([P, 1], F32, name="one")
         nc.scalar.activation(one[:], zeros[:, 0:1], EXP)
 
-        h_bf = held.tile([P, K_IN, NODES], BF16, name="h_bf")
-        nc.vector.tensor_copy(h_bf[:], h_f32[:])
+        identity = held.tile([P, P], F32, name="identity")
+        make_identity(nc, identity[:])
+        self_mask = held.tile([P, P], F32, name="self_mask")
+        nc.vector.tensor_scalar_mul(self_mask[:], identity[:], NEG_BIG)
+
+        h_bf = [held.tile([P, NODES], BF16, name=f"h_bf_{k}") for k in range(K_IN)]
+        wh_ps = [banks.tile([P, NODES], F32, name="bank") for d in range(K_OUT)]
+        for k in range(K_IN):
+            nc.vector.tensor_copy(h_bf[k][:], h_f32[k][:])
+            for d in range(K_OUT):
+                nc.tensor.matmul(wh_ps[d][:], w_sb[k][:, d * P:(d + 1) * P], h_bf[k][:],
+                                 start=(k == 0), stop=(k == K_IN - 1))
         wh_bf = held.tile([P, K_OUT, NODES], BF16, name="wh_bf")
-        for pair in range(K_OUT // 2):
-            wh_ps = banks.tile([P, 2, NODES], F32, name="bank")
-            for half in range(2):
-                d = 2 * pair + half
-                for k in range(K_IN):
-                    nc.tensor.matmul(wh_ps[:, half, :], w_sb[:, k, d * P:(d + 1) * P], h_bf[:, k, :],
-                                     start=(k == 0), stop=(k == K_IN - 1))
-            if pair == 0:
-                nc.vector.tensor_copy(wh_bf[:, 0:2, :], wh_ps[:])
+        for d in range(K_OUT):
+            if d % 2 == 0:
+                nc.vector.tensor_copy(wh_bf[:, d, :], wh_ps[d][:])
             else:
-                nc.scalar.copy(wh_bf[:, 2:4, :], wh_ps[:])
+                nc.scalar.copy(wh_bf[:, d, :], wh_ps[d][:])
 
         p_sb = [held.tile([P, NODES], F32, name=f"p_{c}") for c in range(BLOCKS)]
         q_sb = [held.tile([P, NODES], F32, name=f"q_{c}") for c in range(BLOCKS)]
-        for role, kept in enumerate((p_sb, q_sb)):
-            role_ps = banks.tile([P, BLOCKS, NODES], F32, name="bank")
+        for first_row, kept in ((K_OUT, q_sb), (0, p_sb)):
+            kept_ps = banks.tile([P, BLOCKS, NODES], F32, name="bank")
             for c in range(BLOCKS):
                 for k in range(K_OUT):
-                    nc.tensor.matmul(role_ps[:, c, :], a1_sb[:, role * K_OUT + k, c * P:(c + 1) * P],
+                    nc.tensor.matmul(kept_ps[:, c, :], a1_nodes[:, first_row + k, c * P:(c + 1) * P],
                                      wh_bf[:, k, :], start=(k == 0), stop=(k == K_OUT - 1))
             for c in range(BLOCKS):
-                if role == 0:
-                    nc.vector.tensor_copy(kept[c][:], role_ps[:, c, :])
+                if kept is q_sb:
+                    nc.scalar.copy(kept[c][:], kept_ps[:, c, :])
                 else:
-                    nc.scalar.copy(kept[c][:], role_ps[:, c, :])
+                    nc.vector.tensor_copy(kept[c][:], kept_ps[:, c, :])
 
         e_ps = [scores.tile([P, NODES], F32, name=f"e_{b}") for b in range(BLOCKS)]
 
@@ -113,10 +110,10 @@ def tile_graphattentionlayer_b_kernel(tc, h, W, a1, ef, a3, offs, out):
             r_ps = []
             for c in range(BLOCKS):
                 bank = banks.tile([P, CHUNK], F32, name="bank")
-                first = (t * CHUNK) % EF_COLS
+                first = (t * CHUNK) % GROUP
                 for k in range(K_EDGE):
-                    nc.tensor.matmul(bank[:], a1_sb[:, 2 * K_OUT + k, c * P:(c + 1) * P],
-                                     ef_sb[k][t * CHUNK // EF_COLS][:, first:first + CHUNK],
+                    nc.tensor.matmul(bank[:], a1_edges[:, k, c * P:(c + 1) * P],
+                                     ef_sb[k][t * CHUNK // GROUP][:, first:first + CHUNK],
                                      start=(k == 0), stop=(k == K_EDGE - 1))
                 r_ps.append(bank)
             return r_ps
@@ -167,20 +164,11 @@ def tile_graphattentionlayer_b_kernel(tc, h, W, a1, ef, a3, offs, out):
                 for b in range(PIECE // P):
                     j = (t * CHUNK + piece * PIECE) // P + b
                     for pb in range(BLOCKS):
-                        nc.tensor.matmul(e_ps[pb][:], a3_sb[j // A3_BLOCKS][:, j % A3_BLOCKS, pb * P:(pb + 1) * P],
+                        nc.tensor.matmul(e_ps[pb][:], a3_sb[j * P // GROUP][:, j % (GROUP // P), pb * P:(pb + 1) * P],
                                          nee_t[piece][:, b, :], start=(j == 0), stop=(j == EDGES // P - 1))
 
         qr_next = add_targets(0, project_edges(0))
         r_next = project_edges(1)
-
-        wh_t_bf = held.tile([P, BLOCKS, D_OUT], BF16, name="wh_t_bf")
-        for s in range(BLOCKS):
-            wh_t_ps = flips.tile([P, D_OUT], F32, name="flip")
-            for k in range(K_IN):
-                nc.tensor.matmul(wh_t_ps[:], h_bf[:, k, s * P:(s + 1) * P], w_sb[:, k, :],
-                                 start=(k == 0), stop=(k == K_IN - 1))
-            nc.scalar.copy(wh_t_bf[:, s, :], wh_t_ps[:])
-
         nee_t_last = None
         for t in range(CHUNKS):
             qr_now = qr_next
@@ -194,23 +182,34 @@ def tile_graphattentionlayer_b_kernel(tc, h, W, a1, ef, a3, offs, out):
             nee_t_last = flip(nee_sb)
         mix(CHUNKS - 1, nee_t_last)
 
-        att_t_ps = [flips.tile([P, NODES], F32, name="flip") for c in range(BLOCKS)]
+        scaled = [tail.tile([P, NODES], F32, name="scaled") for pb in range(BLOCKS)]
         for pb in range(BLOCKS):
-            scaled = tail.tile([P, NODES], F32, name="scaled")
-            nc.scalar.mul(scaled[:], e_ps[pb][:], ALPHA)
+            nc.scalar.mul(scaled[pb][:], e_ps[pb][:], ALPHA)
+        weight = [tail.tile([P, NODES], F32, name="weight") for pb in range(BLOCKS)]
+        total = [tail.tile([P, 1], F32, name="total") for pb in range(BLOCKS)]
+        for pb in range(BLOCKS):
             score = tail.tile([P, NODES], F32, name="score")
-            nc.vector.tensor_tensor(score[:], e_ps[pb][:], scaled[:], MAX)
+            nc.vector.tensor_tensor(score[:], e_ps[pb][:], scaled[pb][:], MAX)
             own = score[:, pb * P:(pb + 1) * P]
             nc.vector.tensor_tensor(own, own, self_mask[:], ADD)
             neg_top = tail.tile([P, 1], F32, name="neg_top")
             nc.vector.reduce_max(neg_top[:], score[:], FREE_AXIS, negate=True)
-            weight = tail.tile([P, NODES], F32, name="weight")
-            total = tail.tile([P, 1], F32, name="total")
-            nc.scalar.activation(weight[:], score[:], EXP, bias=neg_top[:], accum_out=total[:])
+            nc.scalar.activation(weight[pb][:], score[:], EXP, bias=neg_top[:], accum_out=total[pb][:])
+
+        wh_t_bf = held.tile([P, BLOCKS, D_OUT], BF16, name="wh_t_bf")
+        for s in range(BLOCKS):
+            wh_t_ps = banks.tile([P, D_OUT], F32, name="bank")
+            for k in range(K_IN):
+                nc.tensor.matmul(wh_t_ps[:], h_bf[k][:, s * P:(s + 1) * P], w_sb[k][:],
+                                 start=(k == 0), stop=(k == K_IN - 1))
+            nc.scalar.copy(wh_t_bf[:, s, :], wh_t_ps[:])
+
+        att_t_ps = [flips.tile([P, NODES], F32, name="flip") for c in range(BLOCKS)]
+        for pb in range(BLOCKS):
             inverse = tail.tile([P, 1], F32, name="inverse")
-            nc.vector.reciprocal(inverse[:], total[:])
+            nc.vector.reciprocal(inverse[:], total[pb][:])
             att = tail.tile([P, NODES], F32, name="att")
-            nc.vector.tensor_scalar_mul(att[:], weight[:], inverse[:])
+            nc.vector.tensor_scalar_mul(att[:], weight[pb][:], inverse[:])
             for c in range(BLOCKS):
                 nc.tensor.transpose(att_t_ps[c][:, pb * P:(pb + 1) * P], att[:, c * P:(c + 1) * P], identity[:])
         att_t_bf = held.tile([P, BLOCKS, NODES], BF16, name="att_t_bf")

@@ -24,6 +24,9 @@ CHUNK = 512
 PIECE = 256
 CHUNKS = EDGES // CHUNK
 PIECES = CHUNK // PIECE
+ALL_PIECES = EDGES // PIECE
+FLIP_LAG = 1
+MIX_LAG = 3
 GROUP = 1024
 WARM_UP = 3
 
@@ -37,7 +40,7 @@ def tile_graphattentionlayer_b_kernel(tc, h, W, a1, ef, a3, offs, out):
         held = pools.enter_context(tc.tile_pool(name="held", bufs=1))
         sums = pools.enter_context(tc.tile_pool(name="sums", bufs=6))
         picked = pools.enter_context(tc.tile_pool(name="picked", bufs=8))
-        flipped = pools.enter_context(tc.tile_pool(name="flipped", bufs=4))
+        flipped = pools.enter_context(tc.tile_pool(name="flipped", bufs=6))
         tail = pools.enter_context(tc.tile_pool(name="tail", bufs=2))
         banks = pools.enter_context(tc.psum_pool(name="banks", bufs=4))
         flips = pools.enter_context(tc.psum_pool(name="flips", bufs=2))
@@ -106,81 +109,84 @@ def tile_graphattentionlayer_b_kernel(tc, h, W, a1, ef, a3, offs, out):
 
         e_ps = [scores.tile([P, NODES], F32, name=f"e_{b}") for b in range(BLOCKS)]
 
-        def project_edges(t):
-            r_ps = []
-            for c in range(BLOCKS):
-                bank = banks.tile([P, CHUNK], F32, name="bank")
-                first = (t * CHUNK) % GROUP
-                for k in range(K_EDGE):
-                    nc.tensor.matmul(bank[:], a1_edges[:, k, c * P:(c + 1) * P],
-                                     ef_sb[k][t * CHUNK // GROUP][:, first:first + CHUNK],
-                                     start=(k == 0), stop=(k == K_EDGE - 1))
-                r_ps.append(bank)
-            return r_ps
+        per_chunk = CHUNK // DEGREE
+        per_piece = PIECE // DEGREE
 
-        def add_targets(t, r_ps):
-            per_chunk = CHUNK // DEGREE
-            by_vector = sums.tile([P, CHUNK], F32, name="qr")
+        def project_edges(t, c):
+            bank = banks.tile([P, CHUNK], F32, name="bank")
+            first = (t * CHUNK) % GROUP
+            for k in range(K_EDGE):
+                nc.tensor.matmul(bank[:], a1_edges[:, k, c * P:(c + 1) * P],
+                                 ef_sb[k][t * CHUNK // GROUP][:, first:first + CHUNK],
+                                 start=(k == 0), stop=(k == K_EDGE - 1))
+            return bank
+
+        def add_targets_on_vector(t, bank):
+            qr = sums.tile([P, CHUNK], F32, name="qr")
             nc.vector.tensor_tensor(
-                by_vector[:].rearrange("p (s e) -> p s e", e=DEGREE),
-                r_ps[0][:].rearrange("p (s e) -> p s e", e=DEGREE),
+                qr[:].rearrange("p (s e) -> p s e", e=DEGREE),
+                bank[:].rearrange("p (s e) -> p s e", e=DEGREE),
                 q_sb[0][:, t * per_chunk:(t + 1) * per_chunk].unsqueeze(2).to_broadcast([P, per_chunk, DEGREE]),
                 ADD)
-            by_scalar = sums.tile([P, CHUNK], F32, name="qr")
-            for s in range(per_chunk):
-                node = t * per_chunk + s
-                nc.scalar.activation(by_scalar[:, s * DEGREE:(s + 1) * DEGREE], r_ps[1][:, s * DEGREE:(s + 1) * DEGREE],
-                                     IDENTITY, bias=q_sb[1][:, node:node + 1])
-            return [by_vector, by_scalar]
+            return qr
 
-        def look_up(t, qr_sb):
+        def add_targets_on_scalar(t, piece, bank, qr):
+            for s in range(piece * per_piece, (piece + 1) * per_piece):
+                node = t * per_chunk + s
+                nc.scalar.activation(qr[:, s * DEGREE:(s + 1) * DEGREE], bank[:, s * DEGREE:(s + 1) * DEGREE],
+                                     IDENTITY, bias=q_sb[1][:, node:node + 1])
+
+        def look_up(u, qr_sb):
+            column = u * PIECE // 16
+            first = (u % PIECES) * PIECE
             nee_sb = []
-            for piece in range(PIECES):
-                column = (t * CHUNK + piece * PIECE) // 16
-                both = []
-                for c in range(BLOCKS):
-                    nee = picked.tile([P, PIECE], F32, name="nee")
-                    nc.vector.tensor_tensor(nee[:], p_sb[c][:].indirect(offsets[:, column:column + PIECE // 16]),
-                                            qr_sb[c][:, piece * PIECE:(piece + 1) * PIECE], ADD)
-                    both.append(nee)
-                nee_sb.append(both)
+            for c in range(BLOCKS):
+                nee = picked.tile([P, PIECE], F32, name="nee")
+                nc.vector.tensor_tensor(nee[:], p_sb[c][:].indirect(offsets[:, column:column + PIECE // 16]),
+                                        qr_sb[c][:, first:first + PIECE], ADD)
+                nee_sb.append(nee)
             return nee_sb
 
         def flip(nee_sb):
-            nee_t = []
-            for piece in range(PIECES):
-                flip_ps = flips.tile([P, PIECE // P, NODES], F32, name="flip")
-                for b in range(PIECE // P):
-                    for c in range(BLOCKS):
-                        nc.tensor.transpose(flip_ps[:, b, c * P:(c + 1) * P], nee_sb[piece][c][:, b * P:(b + 1) * P],
-                                            identity[:])
-                turned = flipped.tile([P, PIECE // P, NODES], BF16, name="turned")
-                nc.scalar.copy(turned[:], flip_ps[:])
-                nee_t.append(turned)
-            return nee_t
+            flip_ps = flips.tile([P, PIECE // P, NODES], F32, name="flip")
+            for b in range(PIECE // P):
+                for c in range(BLOCKS):
+                    nc.tensor.transpose(flip_ps[:, b, c * P:(c + 1) * P], nee_sb[c][:, b * P:(b + 1) * P], identity[:])
+            turned = flipped.tile([P, PIECE // P, NODES], BF16, name="turned")
+            nc.scalar.copy(turned[:], flip_ps[:])
+            return turned
 
-        def mix(t, nee_t):
-            for piece in range(PIECES):
-                for b in range(PIECE // P):
-                    j = (t * CHUNK + piece * PIECE) // P + b
-                    for pb in range(BLOCKS):
-                        nc.tensor.matmul(e_ps[pb][:], a3_sb[j * P // GROUP][:, j % (GROUP // P), pb * P:(pb + 1) * P],
-                                         nee_t[piece][:, b, :], start=(j == 0), stop=(j == EDGES // P - 1))
+        def mix(u, turned):
+            for b in range(PIECE // P):
+                j = u * PIECE // P + b
+                for pb in range(BLOCKS):
+                    nc.tensor.matmul(e_ps[pb][:], a3_sb[j * P // GROUP][:, j % (GROUP // P), pb * P:(pb + 1) * P],
+                                     turned[:, b, :], start=(j == 0), stop=(j == EDGES // P - 1))
 
-        qr_next = add_targets(0, project_edges(0))
-        r_next = project_edges(1)
-        nee_t_last = None
-        for t in range(CHUNKS):
-            qr_now = qr_next
+        r_ps = [[None] * BLOCKS for t in range(CHUNKS)]
+        qr_sb = [None] * CHUNKS
+        nee_sb = [None] * ALL_PIECES
+        nee_t = [None] * ALL_PIECES
+        for t in range(2):
+            for c in range(BLOCKS):
+                r_ps[t][c] = project_edges(t, c)
+        qr_sb[0] = [add_targets_on_vector(0, r_ps[0][0]), sums.tile([P, CHUNK], F32, name="qr")]
+        for piece in range(PIECES):
+            add_targets_on_scalar(0, piece, r_ps[0][1], qr_sb[0][1])
+        for u in range(ALL_PIECES + MIX_LAG):
+            t, piece = divmod(u, PIECES)
             if t + 1 < CHUNKS:
-                qr_next = add_targets(t + 1, r_next)
+                if piece == 0:
+                    qr_sb[t + 1] = [add_targets_on_vector(t + 1, r_ps[t + 1][0]), sums.tile([P, CHUNK], F32, name="qr")]
+                add_targets_on_scalar(t + 1, piece, r_ps[t + 1][1], qr_sb[t + 1][1])
             if t + 2 < CHUNKS:
-                r_next = project_edges(t + 2)
-            nee_sb = look_up(t, qr_now)
-            if t > 0:
-                mix(t - 1, nee_t_last)
-            nee_t_last = flip(nee_sb)
-        mix(CHUNKS - 1, nee_t_last)
+                r_ps[t + 2][piece] = project_edges(t + 2, piece)
+            if u < ALL_PIECES:
+                nee_sb[u] = look_up(u, qr_sb[t])
+            if 0 <= u - FLIP_LAG < ALL_PIECES:
+                nee_t[u - FLIP_LAG] = flip(nee_sb[u - FLIP_LAG])
+            if u >= MIX_LAG:
+                mix(u - MIX_LAG, nee_t[u - MIX_LAG])
 
         scaled = [tail.tile([P, NODES], F32, name="scaled") for pb in range(BLOCKS)]
         for pb in range(BLOCKS):

@@ -8,6 +8,8 @@ BF16 = mybir.dt.bfloat16
 U16 = mybir.dt.uint16
 ADD = mybir.AluOpType.add
 MAX = mybir.AluOpType.max
+MIN = mybir.AluOpType.min
+MULT = mybir.AluOpType.mult
 EXP = mybir.ActivationFunctionType.Exp
 IDENTITY = mybir.ActivationFunctionType.Identity
 FREE_AXIS = mybir.AxisListType.X
@@ -76,8 +78,15 @@ def tile_graphattentionlayer_b_kernel(tc, h, W, a1, ef, a3, offs, out):
 
         identity = held.tile([P, P], F32, name="identity")
         make_identity(nc, identity[:])
-        self_mask = held.tile([P, P], F32, name="self_mask")
-        nc.vector.tensor_scalar_mul(self_mask[:], identity[:], NEG_BIG)
+
+        identity_bf = held.tile([P, P], BF16, name="identity_bf")
+        nc.vector.tensor_copy(identity_bf[:], identity[:])
+        e_ps = [scores.tile([P, NODES], F32, name=f"e_{pb}") for pb in range(BLOCKS)]
+        for pb in range(BLOCKS):
+            self_mask = held.tile([P, NODES], BF16, name=f"self_mask_{pb}")
+            nc.vector.memset(self_mask[:], 0.0)
+            nc.vector.tensor_scalar_mul(self_mask[:, pb * P:(pb + 1) * P], identity[:], NEG_BIG)
+            nc.tensor.matmul(e_ps[pb][:], identity_bf[:], self_mask[:], start=True, stop=False)
 
         h_bf = [held.tile([P, NODES], BF16, name=f"h_bf_{k}") for k in range(K_IN)]
         wh_ps = [banks.tile([P, NODES], F32, name="bank") for d in range(K_OUT)]
@@ -106,8 +115,6 @@ def tile_graphattentionlayer_b_kernel(tc, h, W, a1, ef, a3, offs, out):
                     nc.scalar.copy(kept[c][:], kept_ps[:, c, :])
                 else:
                     nc.vector.tensor_copy(kept[c][:], kept_ps[:, c, :])
-
-        e_ps = [scores.tile([P, NODES], F32, name=f"e_{b}") for b in range(BLOCKS)]
 
         per_chunk = CHUNK // DEGREE
         per_piece = PIECE // DEGREE
@@ -161,7 +168,19 @@ def tile_graphattentionlayer_b_kernel(tc, h, W, a1, ef, a3, offs, out):
                 j = u * PIECE // P + b
                 for pb in range(BLOCKS):
                     nc.tensor.matmul(e_ps[pb][:], a3_sb[j * P // GROUP][:, j % (GROUP // P), pb * P:(pb + 1) * P],
-                                     turned[:, b, :], start=(j == 0), stop=(j == EDGES // P - 1))
+                                     turned[:, b, :], start=False, stop=(j == EDGES // P - 1))
+
+        wh_t_bf = held.tile([P, BLOCKS, D_OUT], BF16, name="wh_t_bf")
+        wh_t_ps = [None] * BLOCKS
+
+        def project_nodes_turned(s, half):
+            if half == 0:
+                wh_t_ps[s] = banks.tile([P, D_OUT], F32, name="bank")
+            for k in range(half * K_IN // 2, (half + 1) * K_IN // 2):
+                nc.tensor.matmul(wh_t_ps[s][:], h_bf[k][:, s * P:(s + 1) * P], w_sb[k][:],
+                                 start=(k == 0), stop=(k == K_IN - 1))
+            if half == 1:
+                nc.scalar.copy(wh_t_bf[:, s, :], wh_t_ps[s][:])
 
         r_ps = [[None] * BLOCKS for t in range(CHUNKS)]
         qr_sb = [None] * CHUNKS
@@ -181,6 +200,8 @@ def tile_graphattentionlayer_b_kernel(tc, h, W, a1, ef, a3, offs, out):
                 add_targets_on_scalar(t + 1, piece, r_ps[t + 1][1], qr_sb[t + 1][1])
             if t + 2 < CHUNKS:
                 r_ps[t + 2][piece] = project_edges(t + 2, piece)
+            elif t < CHUNKS:
+                project_nodes_turned(t + 2 - CHUNKS, piece)
             if u < ALL_PIECES:
                 nee_sb[u] = look_up(u, qr_sb[t])
             if 0 <= u - FLIP_LAG < ALL_PIECES:
@@ -194,46 +215,36 @@ def tile_graphattentionlayer_b_kernel(tc, h, W, a1, ef, a3, offs, out):
         weight = [tail.tile([P, NODES], F32, name="weight") for pb in range(BLOCKS)]
         total = [tail.tile([P, 1], F32, name="total") for pb in range(BLOCKS)]
         for pb in range(BLOCKS):
+            neg_peak = tail.tile([P, 1], F32, name="neg_peak")
+            nc.vector.reduce_max(neg_peak[:], e_ps[pb][:], FREE_AXIS, negate=True)
+            neg_top = tail.tile([P, 1], F32, name="neg_top")
+            nc.vector.scalar_tensor_tensor(neg_top[:], neg_peak[:], ALPHA, neg_peak[:], MULT, MIN)
             score = tail.tile([P, NODES], F32, name="score")
             nc.vector.tensor_tensor(score[:], e_ps[pb][:], scaled[pb][:], MAX)
-            own = score[:, pb * P:(pb + 1) * P]
-            nc.vector.tensor_tensor(own, own, self_mask[:], ADD)
-            neg_top = tail.tile([P, 1], F32, name="neg_top")
-            nc.vector.reduce_max(neg_top[:], score[:], FREE_AXIS, negate=True)
             nc.scalar.activation(weight[pb][:], score[:], EXP, bias=neg_top[:], accum_out=total[pb][:])
 
-        wh_t_bf = held.tile([P, BLOCKS, D_OUT], BF16, name="wh_t_bf")
-        for s in range(BLOCKS):
-            wh_t_ps = banks.tile([P, D_OUT], F32, name="bank")
-            for k in range(K_IN):
-                nc.tensor.matmul(wh_t_ps[:], h_bf[k][:, s * P:(s + 1) * P], w_sb[k][:],
-                                 start=(k == 0), stop=(k == K_IN - 1))
-            nc.scalar.copy(wh_t_bf[:, s, :], wh_t_ps[:])
-
-        att_t_ps = [flips.tile([P, NODES], F32, name="flip") for c in range(BLOCKS)]
+        att_t_ps = [flips.tile([P, BLOCKS, P], F32, name="flip") for pb in range(BLOCKS)]
         for pb in range(BLOCKS):
             inverse = tail.tile([P, 1], F32, name="inverse")
             nc.vector.reciprocal(inverse[:], total[pb][:])
             att = tail.tile([P, NODES], F32, name="att")
             nc.vector.tensor_scalar_mul(att[:], weight[pb][:], inverse[:])
             for c in range(BLOCKS):
-                nc.tensor.transpose(att_t_ps[c][:, pb * P:(pb + 1) * P], att[:, c * P:(c + 1) * P], identity[:])
-        att_t_bf = held.tile([P, BLOCKS, NODES], BF16, name="att_t_bf")
-        nc.vector.tensor_copy(att_t_bf[:, 0, :], att_t_ps[0][:])
-        nc.scalar.copy(att_t_bf[:, 1, :], att_t_ps[1][:])
+                nc.tensor.transpose(att_t_ps[pb][:, c, :], att[:, c * P:(c + 1) * P], identity[:])
+        att_t_bf = [tail.tile([P, BLOCKS, P], BF16, name="att_t_bf") for pb in range(BLOCKS)]
+        nc.vector.tensor_copy(att_t_bf[0][:], att_t_ps[0][:])
+        nc.scalar.copy(att_t_bf[1][:], att_t_ps[1][:])
 
-        out_blocks = out.rearrange("(k p) s -> p k s", p=P)
-        for pair in range(K_OUT // 2):
-            out_ps = banks.tile([P, 2, NODES], F32, name="bank")
-            for half in range(2):
-                d = 2 * pair + half
+        HALF = K_OUT // 2
+        out_ps = [[banks.tile([P, HALF, P], F32, name="bank") for half in range(2)] for pb in range(BLOCKS)]
+        for pb in range(BLOCKS):
+            for d in range(K_OUT):
                 for c in range(BLOCKS):
-                    nc.tensor.matmul(out_ps[:, half, :], wh_t_bf[:, c, d * P:(d + 1) * P], att_t_bf[:, c, :],
-                                     start=(c == 0), stop=(c == BLOCKS - 1))
-            out_sb = tail.tile([P, 2, NODES], F32, name="out_sb")
-            if pair == 0:
-                nc.vector.tensor_copy(out_sb[:], out_ps[:])
-                nc.sync.dma_start(out_blocks[:, 0:2, :], out_sb[:])
-            else:
-                nc.scalar.copy(out_sb[:], out_ps[:])
-                nc.scalar.dma_start(out_blocks[:, 2:4, :], out_sb[:])
+                    nc.tensor.matmul(out_ps[pb][d // HALF][:, d % HALF, :], wh_t_bf[:, c, d * P:(d + 1) * P],
+                                     att_t_bf[pb][:, c, :], start=(c == 0), stop=(c == BLOCKS - 1))
+        out_blocks = out.rearrange("(k p) s -> p k s", p=P)
+        for pb in range(BLOCKS):
+            out_sb = tail.tile([P, K_OUT, P], F32, name="out_sb")
+            nc.vector.tensor_copy(out_sb[:, 0:HALF, :], out_ps[pb][0][:])
+            nc.scalar.copy(out_sb[:, HALF:K_OUT, :], out_ps[pb][1][:])
+            nc.sync.dma_start(out_blocks[:, :, pb * P:(pb + 1) * P], out_sb[:])

@@ -29,7 +29,7 @@ PIECES = CHUNK // PIECE
 ALL_PIECES = EDGES // PIECE
 FLIP_LAG = 1
 MIX_LAG = 3
-GROUP = 1024
+HALF_IN = K_IN // 2
 WARM_UP = 3
 
 FLOPS = 2 * (D_IN * D_OUT * NODES + 2 * D_OUT * NODES * NODES + D_EDGE * NODES * EDGES
@@ -48,25 +48,25 @@ def tile_graphattentionlayer_b_kernel(tc, h, W, a1, ef, a3, offs, out):
         flips = pools.enter_context(tc.psum_pool(name="flips", bufs=2))
         scores = pools.enter_context(tc.psum_pool(name="scores", bufs=1))
 
-        h_f32 = [held.tile([P, NODES], F32, name=f"h_f32_{k}") for k in range(K_IN)]
-        w_sb = [held.tile([P, D_OUT], BF16, name=f"w_{k}") for k in range(K_IN)]
-        for k in range(K_IN):
-            nc.sync.dma_start(h_f32[k][:], h[k * P:(k + 1) * P, :])
-            nc.scalar.dma_start(w_sb[k][:], W[k * P:(k + 1) * P, :])
-        a1_nodes = held.tile([P, 2 * K_OUT, NODES], BF16, name="a1_nodes")
-        nc.scalar.dma_start(a1_nodes[:], a1[0:2 * D_OUT, :].rearrange("(k p) c -> p k c", p=P))
+        h_f32 = [held.tile([P, HALF_IN, NODES], F32, name=f"h_f32_{i}") for i in range(2)]
+        w_sb = [held.tile([P, HALF_IN, D_OUT], BF16, name=f"w_{i}") for i in range(2)]
+        for i in range(2):
+            rows = slice(i * HALF_IN * P, (i + 1) * HALF_IN * P)
+            nc.sync.dma_start(h_f32[i][:], h[rows, :].rearrange("(k p) s -> p k s", p=P))
+            nc.scalar.dma_start(w_sb[i][:], W[rows, :].rearrange("(k p) d -> p k d", p=P))
         a1_edges = held.tile([P, K_EDGE, NODES], BF16, name="a1_edges")
         nc.scalar.dma_start(a1_edges[:], a1[2 * D_OUT:2 * D_OUT + D_EDGE, :].rearrange("(k p) c -> p k c", p=P))
+        a1_nodes = held.tile([P, 2 * K_OUT, NODES], BF16, name="a1_nodes")
+        nc.scalar.dma_start(a1_nodes[:], a1[0:2 * D_OUT, :].rearrange("(k p) c -> p k c", p=P))
         offsets = held.tile([P, EDGES // 16], U16, name="offsets")
-        ef_sb = [[held.tile([P, GROUP], BF16, name=f"ef_{k}_{g}") for g in range(EDGES // GROUP)]
-                 for k in range(K_EDGE)]
-        a3_sb = [held.tile([P, GROUP // P, NODES], BF16, name=f"a3_{g}") for g in range(EDGES // GROUP)]
-        for g in range(EDGES // GROUP):
+        ef_sb = [[held.tile([P, CHUNK], BF16, name=f"ef_{k}_{t}") for t in range(CHUNKS)] for k in range(K_EDGE)]
+        a3_sb = [held.tile([P, CHUNK // P, NODES], BF16, name=f"a3_{t}") for t in range(CHUNKS)]
+        for t in range(CHUNKS):
             for k in range(K_EDGE):
-                nc.sync.dma_start(ef_sb[k][g][:], ef[k * P:(k + 1) * P, g * GROUP:(g + 1) * GROUP])
-            if g == 0:
+                nc.sync.dma_start(ef_sb[k][t][:], ef[k * P:(k + 1) * P, t * CHUNK:(t + 1) * CHUNK])
+            if t == 0:
                 nc.sync.dma_start(offsets[:], offs)
-            nc.sync.dma_start(a3_sb[g][:], a3[g * GROUP:(g + 1) * GROUP, :].rearrange("(b p) s -> p b s", p=P))
+            nc.sync.dma_start(a3_sb[t][:], a3[t * CHUNK:(t + 1) * CHUNK, :].rearrange("(b p) s -> p b s", p=P))
 
         zeros = held.tile([P, CHUNK], BF16, name="zeros")
         nc.vector.memset(zeros[:], 0.0)
@@ -88,13 +88,26 @@ def tile_graphattentionlayer_b_kernel(tc, h, W, a1, ef, a3, offs, out):
             nc.vector.tensor_scalar_mul(self_mask[:, pb * P:(pb + 1) * P], identity[:], NEG_BIG)
             nc.tensor.matmul(e_ps[pb][:], identity_bf[:], self_mask[:], start=True, stop=False)
 
-        h_bf = [held.tile([P, NODES], BF16, name=f"h_bf_{k}") for k in range(K_IN)]
-        wh_ps = [banks.tile([P, NODES], F32, name="bank") for d in range(K_OUT)]
-        for k in range(K_IN):
-            nc.vector.tensor_copy(h_bf[k][:], h_f32[k][:])
-            for d in range(K_OUT):
-                nc.tensor.matmul(wh_ps[d][:], w_sb[k][:, d * P:(d + 1) * P], h_bf[k][:],
-                                 start=(k == 0), stop=(k == K_IN - 1))
+        def project_edges(t, c):
+            bank = banks.tile([P, CHUNK], F32, name="bank")
+            for k in range(K_EDGE):
+                nc.tensor.matmul(bank[:], a1_edges[:, k, c * P:(c + 1) * P], ef_sb[k][t][:],
+                                 start=(k == 0), stop=(k == K_EDGE - 1))
+            return bank
+
+        r_ps = [[None] * BLOCKS for t in range(CHUNKS)]
+
+        h_bf = [held.tile([P, HALF_IN, NODES], BF16, name=f"h_bf_{i}") for i in range(2)]
+        wh_ps = [(banks if d < K_OUT // 2 else flips).tile([P, NODES], F32, name="bank" if d < K_OUT // 2 else "flip")
+                 for d in range(K_OUT)]
+        for i in range(2):
+            nc.vector.tensor_copy(h_bf[i][:], h_f32[i][:])
+            for k in range(HALF_IN):
+                for d in range(K_OUT):
+                    nc.tensor.matmul(wh_ps[d][:], w_sb[i][:, k, d * P:(d + 1) * P], h_bf[i][:, k, :],
+                                     start=(i == 0 and k == 0), stop=(i == 1 and k == HALF_IN - 1))
+        for c in range(BLOCKS):
+            r_ps[0][c] = project_edges(0, c)
         wh_bf = held.tile([P, K_OUT, NODES], BF16, name="wh_bf")
         for d in range(K_OUT):
             if d % 2 == 0:
@@ -102,31 +115,15 @@ def tile_graphattentionlayer_b_kernel(tc, h, W, a1, ef, a3, offs, out):
             else:
                 nc.scalar.copy(wh_bf[:, d, :], wh_ps[d][:])
 
-        p_sb = [held.tile([P, NODES], F32, name=f"p_{c}") for c in range(BLOCKS)]
-        q_sb = [held.tile([P, NODES], F32, name=f"q_{c}") for c in range(BLOCKS)]
-        for first_row, kept in ((K_OUT, q_sb), (0, p_sb)):
-            kept_ps = banks.tile([P, BLOCKS, NODES], F32, name="bank")
-            for c in range(BLOCKS):
-                for k in range(K_OUT):
-                    nc.tensor.matmul(kept_ps[:, c, :], a1_nodes[:, first_row + k, c * P:(c + 1) * P],
-                                     wh_bf[:, k, :], start=(k == 0), stop=(k == K_OUT - 1))
-            for c in range(BLOCKS):
-                if kept is q_sb:
-                    nc.scalar.copy(kept[c][:], kept_ps[:, c, :])
-                else:
-                    nc.vector.tensor_copy(kept[c][:], kept_ps[:, c, :])
+        def project_nodes(first_row, c, pool, tag):
+            product = pool.tile([P, NODES], F32, name=tag)
+            for k in range(K_OUT):
+                nc.tensor.matmul(product[:], a1_nodes[:, first_row + k, c * P:(c + 1) * P], wh_bf[:, k, :],
+                                 start=(k == 0), stop=(k == K_OUT - 1))
+            return product
 
         per_chunk = CHUNK // DEGREE
         per_piece = PIECE // DEGREE
-
-        def project_edges(t, c):
-            bank = banks.tile([P, CHUNK], F32, name="bank")
-            first = (t * CHUNK) % GROUP
-            for k in range(K_EDGE):
-                nc.tensor.matmul(bank[:], a1_edges[:, k, c * P:(c + 1) * P],
-                                 ef_sb[k][t * CHUNK // GROUP][:, first:first + CHUNK],
-                                 start=(k == 0), stop=(k == K_EDGE - 1))
-            return bank
 
         def add_targets_on_vector(t, bank):
             qr = sums.tile([P, CHUNK], F32, name="qr")
@@ -167,7 +164,7 @@ def tile_graphattentionlayer_b_kernel(tc, h, W, a1, ef, a3, offs, out):
             for b in range(PIECE // P):
                 j = u * PIECE // P + b
                 for pb in range(BLOCKS):
-                    nc.tensor.matmul(e_ps[pb][:], a3_sb[j * P // GROUP][:, j % (GROUP // P), pb * P:(pb + 1) * P],
+                    nc.tensor.matmul(e_ps[pb][:], a3_sb[j * P // CHUNK][:, j % (CHUNK // P), pb * P:(pb + 1) * P],
                                      turned[:, b, :], start=False, stop=(j == EDGES // P - 1))
 
         wh_t_bf = held.tile([P, BLOCKS, D_OUT], BF16, name="wh_t_bf")
@@ -176,24 +173,33 @@ def tile_graphattentionlayer_b_kernel(tc, h, W, a1, ef, a3, offs, out):
         def project_nodes_turned(s, half):
             if half == 0:
                 wh_t_ps[s] = banks.tile([P, D_OUT], F32, name="bank")
-            for k in range(half * K_IN // 2, (half + 1) * K_IN // 2):
-                nc.tensor.matmul(wh_t_ps[s][:], h_bf[k][:, s * P:(s + 1) * P], w_sb[k][:],
-                                 start=(k == 0), stop=(k == K_IN - 1))
+            for k in range(HALF_IN):
+                nc.tensor.matmul(wh_t_ps[s][:], h_bf[half][:, k, s * P:(s + 1) * P], w_sb[half][:, k, :],
+                                 start=(half == 0 and k == 0), stop=(half == 1 and k == HALF_IN - 1))
             if half == 1:
                 nc.scalar.copy(wh_t_bf[:, s, :], wh_t_ps[s][:])
 
-        r_ps = [[None] * BLOCKS for t in range(CHUNKS)]
         qr_sb = [None] * CHUNKS
         nee_sb = [None] * ALL_PIECES
         nee_t = [None] * ALL_PIECES
-        for t in range(2):
-            for c in range(BLOCKS):
-                r_ps[t][c] = project_edges(t, c)
+
+        q_sb = [held.tile([P, NODES], F32, name=f"q_{c}") for c in range(BLOCKS)]
+        for c in range(BLOCKS):
+            nc.scalar.copy(q_sb[c][:], project_nodes(K_OUT, c, banks, "bank")[:])
         qr_sb[0] = [add_targets_on_vector(0, r_ps[0][0]), sums.tile([P, CHUNK], F32, name="qr")]
         for piece in range(PIECES):
             add_targets_on_scalar(0, piece, r_ps[0][1], qr_sb[0][1])
+        p_sb = [held.tile([P, NODES], F32, name=f"p_{c}") for c in range(BLOCKS)]
+        p_ps = [project_nodes(0, c, flips, "flip") for c in range(BLOCKS)]
+        nc.vector.tensor_copy(p_sb[0][:], p_ps[0][:])
+        nc.scalar.copy(p_sb[1][:], p_ps[1][:])
+        for c in range(BLOCKS):
+            r_ps[1][c] = project_edges(1, c)
+
         for u in range(ALL_PIECES + MIX_LAG):
             t, piece = divmod(u, PIECES)
+            if u < ALL_PIECES:
+                nee_sb[u] = look_up(u, qr_sb[t])
             if t + 1 < CHUNKS:
                 if piece == 0:
                     qr_sb[t + 1] = [add_targets_on_vector(t + 1, r_ps[t + 1][0]), sums.tile([P, CHUNK], F32, name="qr")]
@@ -202,8 +208,6 @@ def tile_graphattentionlayer_b_kernel(tc, h, W, a1, ef, a3, offs, out):
                 r_ps[t + 2][piece] = project_edges(t + 2, piece)
             elif t < CHUNKS:
                 project_nodes_turned(t + 2 - CHUNKS, piece)
-            if u < ALL_PIECES:
-                nee_sb[u] = look_up(u, qr_sb[t])
             if 0 <= u - FLIP_LAG < ALL_PIECES:
                 nee_t[u - FLIP_LAG] = flip(nee_sb[u - FLIP_LAG])
             if u >= MIX_LAG:

@@ -29,6 +29,7 @@ PIECES = CHUNK // PIECE
 ALL_PIECES = EDGES // PIECE
 FLIP_LAG = 1
 MIX_LAG = 3
+SCALAR_SHARE = 4
 HALF_IN = K_IN // 2
 WARM_UP = 3
 
@@ -124,21 +125,24 @@ def tile_graphattentionlayer_b_kernel(tc, h, W, a1, ef, a3, offs, out):
 
         per_chunk = CHUNK // DEGREE
         per_piece = PIECE // DEGREE
+        for_vector = per_chunk - SCALAR_SHARE
 
         def add_targets_on_vector(t, bank):
             qr = sums.tile([P, CHUNK], F32, name="qr")
             nc.vector.tensor_tensor(
-                qr[:].rearrange("p (s e) -> p s e", e=DEGREE),
-                bank[:].rearrange("p (s e) -> p s e", e=DEGREE),
-                q_sb[0][:, t * per_chunk:(t + 1) * per_chunk].unsqueeze(2).to_broadcast([P, per_chunk, DEGREE]),
+                qr[:, 0:for_vector * DEGREE].rearrange("p (s e) -> p s e", e=DEGREE),
+                bank[:, 0:for_vector * DEGREE].rearrange("p (s e) -> p s e", e=DEGREE),
+                q_sb[0][:, t * per_chunk:t * per_chunk + for_vector].unsqueeze(2).to_broadcast([P, for_vector, DEGREE]),
                 ADD)
             return qr
 
-        def add_targets_on_scalar(t, piece, bank, qr):
-            for s in range(piece * per_piece, (piece + 1) * per_piece):
-                node = t * per_chunk + s
-                nc.scalar.activation(qr[:, s * DEGREE:(s + 1) * DEGREE], bank[:, s * DEGREE:(s + 1) * DEGREE],
-                                     IDENTITY, bias=q_sb[1][:, node:node + 1])
+        def add_targets_on_scalar(t, piece, both_banks, both_qr):
+            for c, first in ((0, for_vector), (1, 0)):
+                for s in range(max(first, piece * per_piece), (piece + 1) * per_piece):
+                    node = t * per_chunk + s
+                    nc.scalar.activation(both_qr[c][:, s * DEGREE:(s + 1) * DEGREE],
+                                         both_banks[c][:, s * DEGREE:(s + 1) * DEGREE],
+                                         IDENTITY, bias=q_sb[c][:, node:node + 1])
 
         def look_up(u, qr_sb):
             column = u * PIECE // 16
@@ -188,7 +192,7 @@ def tile_graphattentionlayer_b_kernel(tc, h, W, a1, ef, a3, offs, out):
             nc.scalar.copy(q_sb[c][:], project_nodes(K_OUT, c, banks, "bank")[:])
         qr_sb[0] = [add_targets_on_vector(0, r_ps[0][0]), sums.tile([P, CHUNK], F32, name="qr")]
         for piece in range(PIECES):
-            add_targets_on_scalar(0, piece, r_ps[0][1], qr_sb[0][1])
+            add_targets_on_scalar(0, piece, r_ps[0], qr_sb[0])
         p_sb = [held.tile([P, NODES], F32, name=f"p_{c}") for c in range(BLOCKS)]
         p_ps = [project_nodes(0, c, flips, "flip") for c in range(BLOCKS)]
         nc.vector.tensor_copy(p_sb[0][:], p_ps[0][:])
@@ -203,7 +207,7 @@ def tile_graphattentionlayer_b_kernel(tc, h, W, a1, ef, a3, offs, out):
             if t + 1 < CHUNKS:
                 if piece == 0:
                     qr_sb[t + 1] = [add_targets_on_vector(t + 1, r_ps[t + 1][0]), sums.tile([P, CHUNK], F32, name="qr")]
-                add_targets_on_scalar(t + 1, piece, r_ps[t + 1][1], qr_sb[t + 1][1])
+                add_targets_on_scalar(t + 1, piece, r_ps[t + 1], qr_sb[t + 1])
             if t + 2 < CHUNKS:
                 r_ps[t + 2][piece] = project_edges(t + 2, piece)
             elif t < CHUNKS:

@@ -82,12 +82,10 @@ def tile_graphattentionlayer_b_kernel(tc, h, W, a1, ef, a3, offs, out):
 
         identity_bf = held.tile([P, P], BF16, name="identity_bf")
         nc.vector.tensor_copy(identity_bf[:], identity[:])
-        e_ps = [scores.tile([P, NODES], F32, name=f"e_{pb}") for pb in range(BLOCKS)]
+        self_mask = [held.tile([P, NODES], BF16, name=f"self_mask_{pb}") for pb in range(BLOCKS)]
         for pb in range(BLOCKS):
-            self_mask = held.tile([P, NODES], BF16, name=f"self_mask_{pb}")
-            nc.vector.memset(self_mask[:], 0.0)
-            nc.vector.tensor_scalar_mul(self_mask[:, pb * P:(pb + 1) * P], identity[:], NEG_BIG)
-            nc.tensor.matmul(e_ps[pb][:], identity_bf[:], self_mask[:], start=True, stop=False)
+            nc.vector.memset(self_mask[pb][:], 0.0)
+            nc.vector.tensor_scalar_mul(self_mask[pb][:, pb * P:(pb + 1) * P], identity[:], NEG_BIG)
 
         def project_edges(t, c):
             bank = banks.tile([P, CHUNK], F32, name="bank")
@@ -172,16 +170,20 @@ def tile_graphattentionlayer_b_kernel(tc, h, W, a1, ef, a3, offs, out):
                                      turned[:, b, :], start=False, stop=(j == EDGES // P - 1))
 
         wh_t_bf = held.tile([P, BLOCKS, D_OUT], BF16, name="wh_t_bf")
-        wh_t_ps = [None] * BLOCKS
 
-        def project_nodes_turned(s, half):
-            if half == 0:
-                wh_t_ps[s] = banks.tile([P, D_OUT], F32, name="bank")
-            for k in range(HALF_IN):
-                nc.tensor.matmul(wh_t_ps[s][:], h_bf[half][:, k, s * P:(s + 1) * P], w_sb[half][:, k, :],
-                                 start=(half == 0 and k == 0), stop=(half == 1 and k == HALF_IN - 1))
-            if half == 1:
-                nc.scalar.copy(wh_t_bf[:, s, :], wh_t_ps[s][:])
+        def project_nodes_turned(s):
+            wh_t_ps = scores.tile([P, D_OUT], F32, name=f"score_{s}")
+            for i in range(2):
+                for k in range(HALF_IN):
+                    nc.tensor.matmul(wh_t_ps[:], h_bf[i][:, k, s * P:(s + 1) * P], w_sb[i][:, k, :],
+                                     start=(i == 0 and k == 0), stop=(i == 1 and k == HALF_IN - 1))
+            nc.scalar.copy(wh_t_bf[:, s, :], wh_t_ps[:])
+
+        e_ps = [None] * BLOCKS
+
+        def open_scores(pb):
+            e_ps[pb] = scores.tile([P, NODES], F32, name=f"score_{pb}")
+            nc.tensor.matmul(e_ps[pb][:], identity_bf[:], self_mask[pb][:], start=True, stop=False)
 
         qr_sb = [None] * CHUNKS
         nee_sb = [None] * ALL_PIECES
@@ -210,10 +212,13 @@ def tile_graphattentionlayer_b_kernel(tc, h, W, a1, ef, a3, offs, out):
                 add_targets_on_scalar(t + 1, piece, r_ps[t + 1], qr_sb[t + 1])
             if t + 2 < CHUNKS:
                 r_ps[t + 2][piece] = project_edges(t + 2, piece)
-            elif t < CHUNKS:
-                project_nodes_turned(t + 2 - CHUNKS, piece)
+            if u < BLOCKS:
+                project_nodes_turned(u)
             if 0 <= u - FLIP_LAG < ALL_PIECES:
                 nee_t[u - FLIP_LAG] = flip(nee_sb[u - FLIP_LAG])
+            if u == MIX_LAG:
+                for pb in range(BLOCKS):
+                    open_scores(pb)
             if u >= MIX_LAG:
                 mix(u - MIX_LAG, nee_t[u - MIX_LAG])
 

@@ -172,7 +172,7 @@ def tile_graphattentionlayer_b_kernel(tc, h, W, a1, ef, a3, offs, out):
         wh_t_bf = held.tile([P, BLOCKS, D_OUT], BF16, name="wh_t_bf")
 
         def project_nodes_turned(s):
-            wh_t_ps = scores.tile([P, D_OUT], F32, name=f"score_{s}")
+            wh_t_ps = banks.tile([P, D_OUT], F32, name="bank")
             for i in range(2):
                 for k in range(HALF_IN):
                     nc.tensor.matmul(wh_t_ps[:], h_bf[i][:, k, s * P:(s + 1) * P], w_sb[i][:, k, :],
@@ -212,8 +212,6 @@ def tile_graphattentionlayer_b_kernel(tc, h, W, a1, ef, a3, offs, out):
                 add_targets_on_scalar(t + 1, piece, r_ps[t + 1], qr_sb[t + 1])
             if t + 2 < CHUNKS:
                 r_ps[t + 2][piece] = project_edges(t + 2, piece)
-            if u < BLOCKS:
-                project_nodes_turned(u)
             if 0 <= u - FLIP_LAG < ALL_PIECES:
                 nee_t[u - FLIP_LAG] = flip(nee_sb[u - FLIP_LAG])
             if u == MIX_LAG:
@@ -235,6 +233,9 @@ def tile_graphattentionlayer_b_kernel(tc, h, W, a1, ef, a3, offs, out):
             score = tail.tile([P, NODES], F32, name="score")
             nc.vector.tensor_tensor(score[:], e_ps[pb][:], scaled[pb][:], MAX)
             nc.scalar.activation(weight[pb][:], score[:], EXP, bias=neg_top[:], accum_out=total[pb][:])
+
+        for s in range(BLOCKS):
+            project_nodes_turned(s)
 
         att_t_ps = [flips.tile([P, BLOCKS, P], F32, name="flip") for pb in range(BLOCKS)]
         for pb in range(BLOCKS):

@@ -29,7 +29,7 @@ PIECES = CHUNK // PIECE
 ALL_PIECES = EDGES // PIECE
 FLIP_LAG = 1
 MIX_LAG = 3
-SCALAR_SHARE = 4
+SCALAR_SHARE = 3
 HALF_IN = K_IN // 2
 WARM_UP = 3
 

@@ -12,7 +12,6 @@ MIN = mybir.AluOpType.min
 MULT = mybir.AluOpType.mult
 EXP = mybir.ActivationFunctionType.Exp
 IDENTITY = mybir.ActivationFunctionType.Identity
-FREE_AXIS = mybir.AxisListType.X
 
 P = 128
 D_IN, D_OUT, D_EDGE = 512, 512, 256
@@ -26,7 +25,10 @@ CHUNK = 512
 PIECE = 256
 CHUNKS = EDGES // CHUNK
 PIECES = CHUNK // PIECE
-ALL_PIECES = EDGES // PIECE
+HALF_PIECE = PIECE // 2
+CUTS = ([(first, PIECE) for first in range(0, EDGES - PIECE, PIECE)]
+        + [(first, HALF_PIECE) for first in range(EDGES - PIECE, EDGES, HALF_PIECE)])
+STEPS = len(CUTS)
 FLIP_LAG = 1
 MIX_LAG = 3
 SCALAR_SHARE = 3
@@ -97,16 +99,15 @@ def tile_graphattentionlayer_b_kernel(tc, h, W, a1, ef, a3, offs, out):
         r_ps = [[None] * BLOCKS for t in range(CHUNKS)]
 
         h_bf = [held.tile([P, HALF_IN, NODES], BF16, name=f"h_bf_{i}") for i in range(2)]
-        wh_ps = [(banks if d < K_OUT // 2 else flips).tile([P, NODES], F32, name="bank" if d < K_OUT // 2 else "flip")
+        wh_ps = [(flips if d < K_OUT // 2 else banks).tile([P, NODES], F32, name="flip" if d < K_OUT // 2 else "bank")
                  for d in range(K_OUT)]
         for i in range(2):
             nc.vector.tensor_copy(h_bf[i][:], h_f32[i][:])
-            for k in range(HALF_IN):
-                for d in range(K_OUT):
+            for d in range(K_OUT):
+                for k in range(HALF_IN):
                     nc.tensor.matmul(wh_ps[d][:], w_sb[i][:, k, d * P:(d + 1) * P], h_bf[i][:, k, :],
                                      start=(i == 0 and k == 0), stop=(i == 1 and k == HALF_IN - 1))
-        for c in range(BLOCKS):
-            r_ps[0][c] = project_edges(0, c)
+        r_ps[0][0] = project_edges(0, 0)
         wh_bf = held.tile([P, K_OUT, NODES], BF16, name="wh_bf")
         for d in range(K_OUT):
             if d % 2 == 0:
@@ -125,46 +126,46 @@ def tile_graphattentionlayer_b_kernel(tc, h, W, a1, ef, a3, offs, out):
         per_piece = PIECE // DEGREE
         for_vector = per_chunk - SCALAR_SHARE
 
-        def add_targets_on_vector(t, bank):
+        def add_targets_on_vector(t, bank, nodes):
             qr = sums.tile([P, CHUNK], F32, name="qr")
             nc.vector.tensor_tensor(
-                qr[:, 0:for_vector * DEGREE].rearrange("p (s e) -> p s e", e=DEGREE),
-                bank[:, 0:for_vector * DEGREE].rearrange("p (s e) -> p s e", e=DEGREE),
-                q_sb[0][:, t * per_chunk:t * per_chunk + for_vector].unsqueeze(2).to_broadcast([P, for_vector, DEGREE]),
+                qr[:, 0:nodes * DEGREE].rearrange("p (s e) -> p s e", e=DEGREE),
+                bank[:, 0:nodes * DEGREE].rearrange("p (s e) -> p s e", e=DEGREE),
+                q_sb[0][:, t * per_chunk:t * per_chunk + nodes].unsqueeze(2).to_broadcast([P, nodes, DEGREE]),
                 ADD)
             return qr
 
-        def add_targets_on_scalar(t, piece, both_banks, both_qr):
-            for c, first in ((0, for_vector), (1, 0)):
+        def add_targets_on_scalar(t, piece, by_vector, both_banks, both_qr):
+            for c, first in ((0, by_vector), (1, 0)):
                 for s in range(max(first, piece * per_piece), (piece + 1) * per_piece):
                     node = t * per_chunk + s
                     nc.scalar.activation(both_qr[c][:, s * DEGREE:(s + 1) * DEGREE],
                                          both_banks[c][:, s * DEGREE:(s + 1) * DEGREE],
                                          IDENTITY, bias=q_sb[c][:, node:node + 1])
 
-        def look_up(u, qr_sb):
-            column = u * PIECE // 16
-            first = (u % PIECES) * PIECE
-            nee_sb = []
-            for c in range(BLOCKS):
-                nee = picked.tile([P, PIECE], F32, name="nee")
-                nc.vector.tensor_tensor(nee[:], p_sb[c][:].indirect(offsets[:, column:column + PIECE // 16]),
-                                        qr_sb[c][:, first:first + PIECE], ADD)
-                nee_sb.append(nee)
-            return nee_sb
+        def look_up(u, c):
+            first, edges = CUTS[u]
+            column = first // 16
+            t, start = divmod(first, CHUNK)
+            nee = picked.tile([P, edges], F32, name="nee")
+            nc.vector.tensor_tensor(nee[:], p_sb[c][:].indirect(offsets[:, column:column + edges // 16]),
+                                    qr_sb[t][c][:, start:start + edges], ADD)
+            return nee
 
-        def flip(nee_sb):
-            flip_ps = flips.tile([P, PIECE // P, NODES], F32, name="flip")
-            for b in range(PIECE // P):
+        def flip(u, nee_sb, pool, tag, copy):
+            edge_blocks = CUTS[u][1] // P
+            flip_ps = pool.tile([P, edge_blocks, NODES], F32, name=tag)
+            for b in range(edge_blocks):
                 for c in range(BLOCKS):
                     nc.tensor.transpose(flip_ps[:, b, c * P:(c + 1) * P], nee_sb[c][:, b * P:(b + 1) * P], identity[:])
-            turned = flipped.tile([P, PIECE // P, NODES], BF16, name="turned")
-            nc.scalar.copy(turned[:], flip_ps[:])
+            turned = flipped.tile([P, edge_blocks, NODES], BF16, name="turned")
+            copy(turned[:], flip_ps[:])
             return turned
 
         def mix(u, turned):
-            for b in range(PIECE // P):
-                j = u * PIECE // P + b
+            first, edges = CUTS[u]
+            for b in range(edges // P):
+                j = first // P + b
                 for pb in range(BLOCKS):
                     nc.tensor.matmul(e_ps[pb][:], a3_sb[j * P // CHUNK][:, j % (CHUNK // P), pb * P:(pb + 1) * P],
                                      turned[:, b, :], start=False, stop=(j == EDGES // P - 1))
@@ -186,52 +187,59 @@ def tile_graphattentionlayer_b_kernel(tc, h, W, a1, ef, a3, offs, out):
             nc.tensor.matmul(e_ps[pb][:], identity_bf[:], self_mask[pb][:], start=True, stop=False)
 
         qr_sb = [None] * CHUNKS
-        nee_sb = [None] * ALL_PIECES
-        nee_t = [None] * ALL_PIECES
+        nee_sb = [[None] * BLOCKS for u in range(STEPS)]
+        nee_t = [None] * STEPS
 
         q_sb = [held.tile([P, NODES], F32, name=f"q_{c}") for c in range(BLOCKS)]
-        for c in range(BLOCKS):
-            nc.scalar.copy(q_sb[c][:], project_nodes(K_OUT, c, banks, "bank")[:])
-        qr_sb[0] = [add_targets_on_vector(0, r_ps[0][0]), sums.tile([P, CHUNK], F32, name="qr")]
-        for piece in range(PIECES):
-            add_targets_on_scalar(0, piece, r_ps[0], qr_sb[0])
         p_sb = [held.tile([P, NODES], F32, name=f"p_{c}") for c in range(BLOCKS)]
-        p_ps = [project_nodes(0, c, flips, "flip") for c in range(BLOCKS)]
-        nc.vector.tensor_copy(p_sb[0][:], p_ps[0][:])
-        nc.scalar.copy(p_sb[1][:], p_ps[1][:])
+        nc.scalar.copy(q_sb[0][:], project_nodes(K_OUT, 0, scores, "score_0")[:])
+        nc.scalar.copy(p_sb[0][:], project_nodes(0, 0, scores, "score_1")[:])
+        qr_sb[0] = [add_targets_on_vector(0, r_ps[0][0], per_chunk), sums.tile([P, CHUNK], F32, name="qr")]
+        for u in range(PIECES):
+            nee_sb[u][0] = look_up(u, 0)
+        r_ps[0][1] = project_edges(0, 1)
+        nc.scalar.copy(q_sb[1][:], project_nodes(K_OUT, 1, flips, "flip")[:])
+        for piece in range(PIECES):
+            add_targets_on_scalar(0, piece, per_chunk, r_ps[0], qr_sb[0])
+        nc.vector.tensor_copy(p_sb[1][:], project_nodes(0, 1, flips, "flip")[:])
+        for u in range(PIECES):
+            nee_sb[u][1] = look_up(u, 1)
         for c in range(BLOCKS):
             r_ps[1][c] = project_edges(1, c)
 
-        for u in range(ALL_PIECES + MIX_LAG):
+        for u in range(STEPS):
             t, piece = divmod(u, PIECES)
-            if u < ALL_PIECES:
-                nee_sb[u] = look_up(u, qr_sb[t])
+            if t > 0:
+                nee_sb[u] = [look_up(u, c) for c in range(BLOCKS)]
             if t + 1 < CHUNKS:
                 if piece == 0:
-                    qr_sb[t + 1] = [add_targets_on_vector(t + 1, r_ps[t + 1][0]), sums.tile([P, CHUNK], F32, name="qr")]
-                add_targets_on_scalar(t + 1, piece, r_ps[t + 1], qr_sb[t + 1])
+                    qr_sb[t + 1] = [add_targets_on_vector(t + 1, r_ps[t + 1][0], for_vector), sums.tile([P, CHUNK], F32, name="qr")]
+                add_targets_on_scalar(t + 1, piece, for_vector, r_ps[t + 1], qr_sb[t + 1])
             if t + 2 < CHUNKS:
                 r_ps[t + 2][piece] = project_edges(t + 2, piece)
-            if 0 <= u - FLIP_LAG < ALL_PIECES:
-                nee_t[u - FLIP_LAG] = flip(nee_sb[u - FLIP_LAG])
+            if u >= FLIP_LAG:
+                copy = nc.scalar.copy if u < STEPS - 1 else nc.vector.tensor_copy
+                nee_t[u - FLIP_LAG] = flip(u - FLIP_LAG, nee_sb[u - FLIP_LAG], flips, "flip", copy)
             if u == MIX_LAG:
                 for pb in range(BLOCKS):
                     open_scores(pb)
             if u >= MIX_LAG:
                 mix(u - MIX_LAG, nee_t[u - MIX_LAG])
 
-        scaled = [tail.tile([P, NODES], F32, name="scaled") for pb in range(BLOCKS)]
-        for pb in range(BLOCKS):
-            nc.scalar.mul(scaled[pb][:], e_ps[pb][:], ALPHA)
+        nee_t[STEPS - 1] = flip(STEPS - 1, nee_sb[STEPS - 1], banks, "bank", nc.scalar.copy)
+        for u in range(STEPS - MIX_LAG, STEPS):
+            mix(u, nee_t[u])
+
         weight = [tail.tile([P, NODES], F32, name="weight") for pb in range(BLOCKS)]
         total = [tail.tile([P, 1], F32, name="total") for pb in range(BLOCKS)]
         for pb in range(BLOCKS):
+            neg_scaled = tail.tile([P, NODES], F32, name="neg_scaled")
             neg_peak = tail.tile([P, 1], F32, name="neg_peak")
-            nc.vector.reduce_max(neg_peak[:], e_ps[pb][:], FREE_AXIS, negate=True)
+            nc.vector.tensor_scalar(neg_scaled[:], e_ps[pb][:], -ALPHA, None, MULT, MIN, accum_out=neg_peak[:])
             neg_top = tail.tile([P, 1], F32, name="neg_top")
-            nc.vector.scalar_tensor_tensor(neg_top[:], neg_peak[:], ALPHA, neg_peak[:], MULT, MIN)
+            nc.vector.scalar_tensor_tensor(neg_top[:], neg_peak[:], 1.0 / ALPHA, neg_peak[:], MULT, MIN)
             score = tail.tile([P, NODES], F32, name="score")
-            nc.vector.tensor_tensor(score[:], e_ps[pb][:], scaled[pb][:], MAX)
+            nc.vector.scalar_tensor_tensor(score[:], neg_scaled[:], -1.0, e_ps[pb][:], MULT, MAX)
             nc.scalar.activation(weight[pb][:], score[:], EXP, bias=neg_top[:], accum_out=total[pb][:])
 
         for s in range(BLOCKS):

@@ -31,7 +31,7 @@ CUTS = ([(first, PIECE) for first in range(0, EDGES - PIECE, PIECE)]
 STEPS = len(CUTS)
 FLIP_LAG = 1
 MIX_LAG = 3
-SCALAR_SHARE = 3
+SCALAR_TURN = 2
 HALF_IN = K_IN // 2
 WARM_UP = 3
 
@@ -48,7 +48,7 @@ def tile_graphattentionlayer_b_kernel(tc, h, W, a1, ef, a3, offs, out):
         flipped = pools.enter_context(tc.tile_pool(name="flipped", bufs=6))
         tail = pools.enter_context(tc.tile_pool(name="tail", bufs=2))
         banks = pools.enter_context(tc.psum_pool(name="banks", bufs=4))
-        flips = pools.enter_context(tc.psum_pool(name="flips", bufs=2))
+        flips = pools.enter_context(tc.psum_pool(name="flips", bufs=3))
         scores = pools.enter_context(tc.psum_pool(name="scores", bufs=1))
 
         h_f32 = [held.tile([P, HALF_IN, NODES], F32, name=f"h_f32_{i}") for i in range(2)]
@@ -84,10 +84,10 @@ def tile_graphattentionlayer_b_kernel(tc, h, W, a1, ef, a3, offs, out):
 
         identity_bf = held.tile([P, P], BF16, name="identity_bf")
         nc.vector.tensor_copy(identity_bf[:], identity[:])
-        self_mask = [held.tile([P, NODES], BF16, name=f"self_mask_{pb}") for pb in range(BLOCKS)]
+        self_mask = held.tile([P, BLOCKS, NODES], BF16, name="self_mask")
+        nc.vector.memset(self_mask[:], 0.0)
         for pb in range(BLOCKS):
-            nc.vector.memset(self_mask[pb][:], 0.0)
-            nc.vector.tensor_scalar_mul(self_mask[pb][:, pb * P:(pb + 1) * P], identity[:], NEG_BIG)
+            nc.vector.tensor_scalar_mul(self_mask[:, pb, pb * P:(pb + 1) * P], identity[:], NEG_BIG)
 
         def project_edges(t, c):
             bank = banks.tile([P, CHUNK], F32, name="bank")
@@ -124,24 +124,19 @@ def tile_graphattentionlayer_b_kernel(tc, h, W, a1, ef, a3, offs, out):
 
         per_chunk = CHUNK // DEGREE
         per_piece = PIECE // DEGREE
-        for_vector = per_chunk - SCALAR_SHARE
 
-        def add_targets_on_vector(t, bank, nodes):
-            qr = sums.tile([P, CHUNK], F32, name="qr")
+        def add_targets_on_vector(t, c):
             nc.vector.tensor_tensor(
-                qr[:, 0:nodes * DEGREE].rearrange("p (s e) -> p s e", e=DEGREE),
-                bank[:, 0:nodes * DEGREE].rearrange("p (s e) -> p s e", e=DEGREE),
-                q_sb[0][:, t * per_chunk:t * per_chunk + nodes].unsqueeze(2).to_broadcast([P, nodes, DEGREE]),
+                qr_sb[t][c][:].rearrange("p (s e) -> p s e", e=DEGREE),
+                r_ps[t][c][:].rearrange("p (s e) -> p s e", e=DEGREE),
+                q_sb[c][:, t * per_chunk:(t + 1) * per_chunk].unsqueeze(2).to_broadcast([P, per_chunk, DEGREE]),
                 ADD)
-            return qr
 
-        def add_targets_on_scalar(t, piece, by_vector, both_banks, both_qr):
-            for c, first in ((0, by_vector), (1, 0)):
-                for s in range(max(first, piece * per_piece), (piece + 1) * per_piece):
-                    node = t * per_chunk + s
-                    nc.scalar.activation(both_qr[c][:, s * DEGREE:(s + 1) * DEGREE],
-                                         both_banks[c][:, s * DEGREE:(s + 1) * DEGREE],
-                                         IDENTITY, bias=q_sb[c][:, node:node + 1])
+        def add_targets_on_scalar(t, c, piece):
+            for s in range(piece * per_piece, (piece + 1) * per_piece):
+                node = t * per_chunk + s
+                nc.scalar.activation(qr_sb[t][c][:, s * DEGREE:(s + 1) * DEGREE], r_ps[t][c][:, s * DEGREE:(s + 1) * DEGREE],
+                                     IDENTITY, bias=q_sb[c][:, node:node + 1])
 
         def look_up(u, c):
             first, edges = CUTS[u]
@@ -167,8 +162,8 @@ def tile_graphattentionlayer_b_kernel(tc, h, W, a1, ef, a3, offs, out):
             for b in range(edges // P):
                 j = first // P + b
                 for pb in range(BLOCKS):
-                    nc.tensor.matmul(e_ps[pb][:], a3_sb[j * P // CHUNK][:, j % (CHUNK // P), pb * P:(pb + 1) * P],
-                                     turned[:, b, :], start=False, stop=(j == EDGES // P - 1))
+                    nc.tensor.matmul(e_ps[:, pb, :], a3_sb[j * P // CHUNK][:, j % (CHUNK // P), pb * P:(pb + 1) * P],
+                                     turned[:, b, :], start=False, stop=(j == EDGES // P - 1 and pb == BLOCKS - 1))
 
         wh_t_bf = held.tile([P, BLOCKS, D_OUT], BF16, name="wh_t_bf")
 
@@ -180,27 +175,27 @@ def tile_graphattentionlayer_b_kernel(tc, h, W, a1, ef, a3, offs, out):
                                      start=(i == 0 and k == 0), stop=(i == 1 and k == HALF_IN - 1))
             nc.scalar.copy(wh_t_bf[:, s, :], wh_t_ps[:])
 
-        e_ps = [None] * BLOCKS
+        def open_scores():
+            bank = scores.tile([P, BLOCKS, NODES], F32, name="score")
+            nc.tensor.matmul(bank[:], identity_bf[:], self_mask[:], start=True, stop=False)
+            return bank
 
-        def open_scores(pb):
-            e_ps[pb] = scores.tile([P, NODES], F32, name=f"score_{pb}")
-            nc.tensor.matmul(e_ps[pb][:], identity_bf[:], self_mask[pb][:], start=True, stop=False)
-
-        qr_sb = [None] * CHUNKS
+        qr_sb = [[None] * BLOCKS for t in range(CHUNKS)]
         nee_sb = [[None] * BLOCKS for u in range(STEPS)]
         nee_t = [None] * STEPS
 
         q_sb = [held.tile([P, NODES], F32, name=f"q_{c}") for c in range(BLOCKS)]
         p_sb = [held.tile([P, NODES], F32, name=f"p_{c}") for c in range(BLOCKS)]
-        nc.scalar.copy(q_sb[0][:], project_nodes(K_OUT, 0, scores, "score_0")[:])
-        nc.scalar.copy(p_sb[0][:], project_nodes(0, 0, scores, "score_1")[:])
-        qr_sb[0] = [add_targets_on_vector(0, r_ps[0][0], per_chunk), sums.tile([P, CHUNK], F32, name="qr")]
+        nc.scalar.copy(q_sb[0][:], project_nodes(K_OUT, 0, scores, "score")[:])
+        nc.scalar.copy(p_sb[0][:], project_nodes(0, 0, flips, "flip")[:])
+        qr_sb[0] = [sums.tile([P, CHUNK], F32, name="qr") for c in range(BLOCKS)]
+        add_targets_on_vector(0, 0)
         for u in range(PIECES):
             nee_sb[u][0] = look_up(u, 0)
         r_ps[0][1] = project_edges(0, 1)
         nc.scalar.copy(q_sb[1][:], project_nodes(K_OUT, 1, flips, "flip")[:])
         for piece in range(PIECES):
-            add_targets_on_scalar(0, piece, per_chunk, r_ps[0], qr_sb[0])
+            add_targets_on_scalar(0, 1, piece)
         nc.vector.tensor_copy(p_sb[1][:], project_nodes(0, 1, flips, "flip")[:])
         for u in range(PIECES):
             nee_sb[u][1] = look_up(u, 1)
@@ -212,17 +207,20 @@ def tile_graphattentionlayer_b_kernel(tc, h, W, a1, ef, a3, offs, out):
             if t > 0:
                 nee_sb[u] = [look_up(u, c) for c in range(BLOCKS)]
             if t + 1 < CHUNKS:
+                scalar_alone = (t + 1) % SCALAR_TURN == 0
                 if piece == 0:
-                    qr_sb[t + 1] = [add_targets_on_vector(t + 1, r_ps[t + 1][0], for_vector), sums.tile([P, CHUNK], F32, name="qr")]
-                add_targets_on_scalar(t + 1, piece, for_vector, r_ps[t + 1], qr_sb[t + 1])
+                    qr_sb[t + 1] = [sums.tile([P, CHUNK], F32, name="qr") for c in range(BLOCKS)]
+                    if not scalar_alone:
+                        add_targets_on_vector(t + 1, 0)
+                for c in range(0 if scalar_alone else 1, BLOCKS):
+                    add_targets_on_scalar(t + 1, c, piece)
             if t + 2 < CHUNKS:
                 r_ps[t + 2][piece] = project_edges(t + 2, piece)
             if u >= FLIP_LAG:
                 copy = nc.scalar.copy if u < STEPS - 1 else nc.vector.tensor_copy
                 nee_t[u - FLIP_LAG] = flip(u - FLIP_LAG, nee_sb[u - FLIP_LAG], flips, "flip", copy)
             if u == MIX_LAG:
-                for pb in range(BLOCKS):
-                    open_scores(pb)
+                e_ps = open_scores()
             if u >= MIX_LAG:
                 mix(u - MIX_LAG, nee_t[u - MIX_LAG])
 
@@ -232,15 +230,16 @@ def tile_graphattentionlayer_b_kernel(tc, h, W, a1, ef, a3, offs, out):
 
         weight = [tail.tile([P, NODES], F32, name="weight") for pb in range(BLOCKS)]
         total = [tail.tile([P, 1], F32, name="total") for pb in range(BLOCKS)]
+        neg_scaled = [tail.tile([P, NODES], F32, name="neg_scaled") for pb in range(BLOCKS)]
+        neg_peak = [tail.tile([P, 1], F32, name="neg_peak") for pb in range(BLOCKS)]
+        neg_top = [tail.tile([P, 1], F32, name="neg_top") for pb in range(BLOCKS)]
+        score = [tail.tile([P, NODES], F32, name="score") for pb in range(BLOCKS)]
         for pb in range(BLOCKS):
-            neg_scaled = tail.tile([P, NODES], F32, name="neg_scaled")
-            neg_peak = tail.tile([P, 1], F32, name="neg_peak")
-            nc.vector.tensor_scalar(neg_scaled[:], e_ps[pb][:], -ALPHA, None, MULT, MIN, accum_out=neg_peak[:])
-            neg_top = tail.tile([P, 1], F32, name="neg_top")
-            nc.vector.scalar_tensor_tensor(neg_top[:], neg_peak[:], 1.0 / ALPHA, neg_peak[:], MULT, MIN)
-            score = tail.tile([P, NODES], F32, name="score")
-            nc.vector.scalar_tensor_tensor(score[:], neg_scaled[:], -1.0, e_ps[pb][:], MULT, MAX)
-            nc.scalar.activation(weight[pb][:], score[:], EXP, bias=neg_top[:], accum_out=total[pb][:])
+            nc.vector.tensor_scalar(neg_scaled[pb][:], e_ps[:, pb, :], -ALPHA, None, MULT, MIN, accum_out=neg_peak[pb][:])
+        for pb in range(BLOCKS):
+            nc.vector.scalar_tensor_tensor(neg_top[pb][:], neg_peak[pb][:], 1.0 / ALPHA, neg_peak[pb][:], MULT, MIN)
+            nc.vector.scalar_tensor_tensor(score[pb][:], neg_scaled[pb][:], -1.0, e_ps[:, pb, :], MULT, MAX)
+            nc.scalar.activation(weight[pb][:], score[pb][:], EXP, bias=neg_top[pb][:], accum_out=total[pb][:])
 
         for s in range(BLOCKS):
             project_nodes_turned(s)

@@ -31,7 +31,7 @@ CUTS = ([(first, PIECE) for first in range(0, EDGES - PIECE, PIECE)]
 STEPS = len(CUTS)
 FLIP_LAG = 1
 MIX_LAG = 3
-SCALAR_TURN = 2
+SCALAR_TURN = 1
 HALF_IN = K_IN // 2
 WARM_UP = 3
 

@@ -31,7 +31,7 @@ CUTS = ([(first, PIECE) for first in range(0, EDGES - PIECE, PIECE)]
 STEPS = len(CUTS)
 FLIP_LAG = 1
 MIX_LAG = 3
-SCALAR_TURN = 1
+VECTOR_TURN = 4
 HALF_IN = K_IN // 2
 WARM_UP = 3
 
@@ -125,11 +125,13 @@ def tile_graphattentionlayer_b_kernel(tc, h, W, a1, ef, a3, offs, out):
         per_chunk = CHUNK // DEGREE
         per_piece = PIECE // DEGREE
 
-        def add_targets_on_vector(t, c):
+        def add_targets_on_vector(t, c, piece):
+            edges = slice(piece * PIECE, (piece + 1) * PIECE)
+            node = t * per_chunk + piece * per_piece
             nc.vector.tensor_tensor(
-                qr_sb[t][c][:].rearrange("p (s e) -> p s e", e=DEGREE),
-                r_ps[t][c][:].rearrange("p (s e) -> p s e", e=DEGREE),
-                q_sb[c][:, t * per_chunk:(t + 1) * per_chunk].unsqueeze(2).to_broadcast([P, per_chunk, DEGREE]),
+                qr_sb[t][c][:, edges].rearrange("p (s e) -> p s e", e=DEGREE),
+                r_ps[t][c][:, edges].rearrange("p (s e) -> p s e", e=DEGREE),
+                q_sb[c][:, node:node + per_piece].unsqueeze(2).to_broadcast([P, per_piece, DEGREE]),
                 ADD)
 
         def add_targets_on_scalar(t, c, piece):
@@ -186,33 +188,38 @@ def tile_graphattentionlayer_b_kernel(tc, h, W, a1, ef, a3, offs, out):
 
         q_sb = [held.tile([P, NODES], F32, name=f"q_{c}") for c in range(BLOCKS)]
         p_sb = [held.tile([P, NODES], F32, name=f"p_{c}") for c in range(BLOCKS)]
-        nc.scalar.copy(q_sb[0][:], project_nodes(K_OUT, 0, scores, "score")[:])
+        nc.vector.tensor_copy(q_sb[0][:], project_nodes(K_OUT, 0, scores, "score")[:])
         nc.scalar.copy(p_sb[0][:], project_nodes(0, 0, flips, "flip")[:])
-        qr_sb[0] = [sums.tile([P, CHUNK], F32, name="qr") for c in range(BLOCKS)]
-        add_targets_on_vector(0, 0)
-        for u in range(PIECES):
-            nee_sb[u][0] = look_up(u, 0)
+        for t in range(2):
+            qr_sb[t] = [sums.tile([P, CHUNK], F32, name="qr") for c in range(BLOCKS)]
+        for piece in range(PIECES):
+            add_targets_on_vector(0, 0, piece)
+        nee_sb[0][0] = look_up(0, 0)
         r_ps[0][1] = project_edges(0, 1)
         nc.scalar.copy(q_sb[1][:], project_nodes(K_OUT, 1, flips, "flip")[:])
         for piece in range(PIECES):
             add_targets_on_scalar(0, 1, piece)
-        nc.vector.tensor_copy(p_sb[1][:], project_nodes(0, 1, flips, "flip")[:])
-        for u in range(PIECES):
-            nee_sb[u][1] = look_up(u, 1)
+        p_ps = project_nodes(0, 1, flips, "flip")
         for c in range(BLOCKS):
             r_ps[1][c] = project_edges(1, c)
+        nc.vector.tensor_copy(p_sb[1][:], p_ps[:])
+        nee_sb[1][0] = look_up(1, 0)
+        for piece in range(PIECES):
+            add_targets_on_vector(1, 0, piece)
+        for u in range(PIECES):
+            nee_sb[u][1] = look_up(u, 1)
 
         for u in range(STEPS):
             t, piece = divmod(u, PIECES)
             if t > 0:
                 nee_sb[u] = [look_up(u, c) for c in range(BLOCKS)]
             if t + 1 < CHUNKS:
-                scalar_alone = (t + 1) % SCALAR_TURN == 0
-                if piece == 0:
+                vector_helps = (t + 1) % VECTOR_TURN == 1
+                if piece == 0 and t > 0:
                     qr_sb[t + 1] = [sums.tile([P, CHUNK], F32, name="qr") for c in range(BLOCKS)]
-                    if not scalar_alone:
-                        add_targets_on_vector(t + 1, 0)
-                for c in range(0 if scalar_alone else 1, BLOCKS):
+                if vector_helps and t > 0:
+                    add_targets_on_vector(t + 1, 0, piece)
+                for c in range(1 if vector_helps else 0, BLOCKS):
                     add_targets_on_scalar(t + 1, c, piece)
             if t + 2 < CHUNKS:
                 r_ps[t + 2][piece] = project_edges(t + 2, piece)
@@ -244,17 +251,17 @@ def tile_graphattentionlayer_b_kernel(tc, h, W, a1, ef, a3, offs, out):
         for s in range(BLOCKS):
             project_nodes_turned(s)
 
-        att_t_ps = [flips.tile([P, BLOCKS, P], F32, name="flip") for pb in range(BLOCKS)]
+        att_t_ps = [flips.tile([P, BLOCKS, P], BF16, name="flip") for pb in range(BLOCKS)]
         for pb in range(BLOCKS):
             inverse = tail.tile([P, 1], F32, name="inverse")
             nc.vector.reciprocal(inverse[:], total[pb][:])
-            att = tail.tile([P, NODES], F32, name="att")
+            att = tail.tile([P, NODES], BF16, name="att")
             nc.vector.tensor_scalar_mul(att[:], weight[pb][:], inverse[:])
             for c in range(BLOCKS):
-                nc.tensor.transpose(att_t_ps[pb][:, c, :], att[:, c * P:(c + 1) * P], identity[:])
+                nc.tensor.transpose(att_t_ps[pb][:, c, :], att[:, c * P:(c + 1) * P], identity_bf[:])
         att_t_bf = [tail.tile([P, BLOCKS, P], BF16, name="att_t_bf") for pb in range(BLOCKS)]
-        nc.vector.tensor_copy(att_t_bf[0][:], att_t_ps[0][:])
-        nc.scalar.copy(att_t_bf[1][:], att_t_ps[1][:])
+        for pb in range(BLOCKS):
+            nc.vector.tensor_copy(att_t_bf[pb][:], att_t_ps[pb][:])
 
         HALF = K_OUT // 2
         out_ps = [[banks.tile([P, HALF, P], F32, name="bank") for half in range(2)] for pb in range(BLOCKS)]

@@ -43,9 +43,9 @@ def tile_graphattentionlayer_b_kernel(tc, h, W, a1, ef, a3, offs, out):
     nc = tc.nc
     with ExitStack() as pools:
         held = pools.enter_context(tc.tile_pool(name="held", bufs=1))
-        sums = pools.enter_context(tc.tile_pool(name="sums", bufs=6))
-        picked = pools.enter_context(tc.tile_pool(name="picked", bufs=8))
-        flipped = pools.enter_context(tc.tile_pool(name="flipped", bufs=6))
+        sums = pools.enter_context(tc.tile_pool(name="sums", bufs=8))
+        picked = pools.enter_context(tc.tile_pool(name="picked", bufs=16))
+        flipped = pools.enter_context(tc.tile_pool(name="flipped", bufs=8))
         tail = pools.enter_context(tc.tile_pool(name="tail", bufs=2))
         banks = pools.enter_context(tc.psum_pool(name="banks", bufs=4))
         flips = pools.enter_context(tc.psum_pool(name="flips", bufs=3))
@@ -273,6 +273,7 @@ def tile_graphattentionlayer_b_kernel(tc, h, W, a1, ef, a3, offs, out):
         out_blocks = out.rearrange("(k p) s -> p k s", p=P)
         for pb in range(BLOCKS):
             out_sb = tail.tile([P, K_OUT, P], F32, name="out_sb")
-            nc.vector.tensor_copy(out_sb[:, 0:HALF, :], out_ps[pb][0][:])
-            nc.scalar.copy(out_sb[:, HALF:K_OUT, :], out_ps[pb][1][:])
-            nc.sync.dma_start(out_blocks[:, :, pb * P:(pb + 1) * P], out_sb[:])
+            nc.scalar.copy(out_sb[:, 0:HALF, :], out_ps[pb][0][:])
+            nc.vector.tensor_copy(out_sb[:, HALF:K_OUT, :], out_ps[pb][1][:])
+            nc.scalar.dma_start(out_blocks[:, 0:HALF, pb * P:(pb + 1) * P], out_sb[:, 0:HALF, :])
+            nc.sync.dma_start(out_blocks[:, HALF:K_OUT, pb * P:(pb + 1) * P], out_sb[:, HALF:K_OUT, :])

@@ -31,7 +31,7 @@ CUTS = ([(first, PIECE) for first in range(0, EDGES - PIECE, PIECE)]
 STEPS = len(CUTS)
 FLIP_LAG = 1
 MIX_LAG = 3
-VECTOR_TURN = 4
+VECTOR_SHARE = 4
 HALF_IN = K_IN // 2
 WARM_UP = 3
 
@@ -125,17 +125,17 @@ def tile_graphattentionlayer_b_kernel(tc, h, W, a1, ef, a3, offs, out):
         per_chunk = CHUNK // DEGREE
         per_piece = PIECE // DEGREE
 
-        def add_targets_on_vector(t, c, piece):
-            edges = slice(piece * PIECE, (piece + 1) * PIECE)
-            node = t * per_chunk + piece * per_piece
+        def add_targets_on_vector(t, c, first, end):
+            edges = slice(first * DEGREE, end * DEGREE)
+            nodes = slice(t * per_chunk + first, t * per_chunk + end)
             nc.vector.tensor_tensor(
                 qr_sb[t][c][:, edges].rearrange("p (s e) -> p s e", e=DEGREE),
                 r_ps[t][c][:, edges].rearrange("p (s e) -> p s e", e=DEGREE),
-                q_sb[c][:, node:node + per_piece].unsqueeze(2).to_broadcast([P, per_piece, DEGREE]),
+                q_sb[c][:, nodes].unsqueeze(2).to_broadcast([P, end - first, DEGREE]),
                 ADD)
 
-        def add_targets_on_scalar(t, c, piece):
-            for s in range(piece * per_piece, (piece + 1) * per_piece):
+        def add_targets_on_scalar(t, c, first, end):
+            for s in range(first, end):
                 node = t * per_chunk + s
                 nc.scalar.activation(qr_sb[t][c][:, s * DEGREE:(s + 1) * DEGREE], r_ps[t][c][:, s * DEGREE:(s + 1) * DEGREE],
                                      IDENTITY, bias=q_sb[c][:, node:node + 1])
@@ -190,22 +190,18 @@ def tile_graphattentionlayer_b_kernel(tc, h, W, a1, ef, a3, offs, out):
         p_sb = [held.tile([P, NODES], F32, name=f"p_{c}") for c in range(BLOCKS)]
         nc.vector.tensor_copy(q_sb[0][:], project_nodes(K_OUT, 0, scores, "score")[:])
         nc.scalar.copy(p_sb[0][:], project_nodes(0, 0, flips, "flip")[:])
-        for t in range(2):
-            qr_sb[t] = [sums.tile([P, CHUNK], F32, name="qr") for c in range(BLOCKS)]
+        qr_sb[0] = [sums.tile([P, CHUNK], F32, name="qr") for c in range(BLOCKS)]
         for piece in range(PIECES):
-            add_targets_on_vector(0, 0, piece)
+            add_targets_on_vector(0, 0, piece * per_piece, (piece + 1) * per_piece)
         nee_sb[0][0] = look_up(0, 0)
         r_ps[0][1] = project_edges(0, 1)
         nc.scalar.copy(q_sb[1][:], project_nodes(K_OUT, 1, flips, "flip")[:])
-        for piece in range(PIECES):
-            add_targets_on_scalar(0, 1, piece)
+        add_targets_on_scalar(0, 1, 0, per_chunk)
         p_ps = project_nodes(0, 1, flips, "flip")
         for c in range(BLOCKS):
             r_ps[1][c] = project_edges(1, c)
         nc.vector.tensor_copy(p_sb[1][:], p_ps[:])
         nee_sb[1][0] = look_up(1, 0)
-        for piece in range(PIECES):
-            add_targets_on_vector(1, 0, piece)
         for u in range(PIECES):
             nee_sb[u][1] = look_up(u, 1)
 
@@ -214,13 +210,12 @@ def tile_graphattentionlayer_b_kernel(tc, h, W, a1, ef, a3, offs, out):
             if t > 0:
                 nee_sb[u] = [look_up(u, c) for c in range(BLOCKS)]
             if t + 1 < CHUNKS:
-                vector_helps = (t + 1) % VECTOR_TURN == 1
-                if piece == 0 and t > 0:
+                if piece == 0:
                     qr_sb[t + 1] = [sums.tile([P, CHUNK], F32, name="qr") for c in range(BLOCKS)]
-                if vector_helps and t > 0:
-                    add_targets_on_vector(t + 1, 0, piece)
-                for c in range(1 if vector_helps else 0, BLOCKS):
-                    add_targets_on_scalar(t + 1, c, piece)
+                for c, by_scalar in ((0, per_chunk - VECTOR_SHARE), (1, per_chunk)):
+                    add_targets_on_scalar(t + 1, c, piece * per_piece, min((piece + 1) * per_piece, by_scalar))
+                if piece == PIECES - 1:
+                    add_targets_on_vector(t + 1, 0, per_chunk - VECTOR_SHARE, per_chunk)
             if t + 2 < CHUNKS:
                 r_ps[t + 2][piece] = project_edges(t + 2, piece)
             if u >= FLIP_LAG:

@@ -33,7 +33,6 @@ FLIP_LAG = 1
 MIX_LAG = 3
 VECTOR_SHARE = 4
 HALF_IN = K_IN // 2
-WARM_UP = 3
 
 FLOPS = 2 * (D_IN * D_OUT * NODES + 2 * D_OUT * NODES * NODES + D_EDGE * NODES * EDGES
              + EDGES * NODES * NODES + NODES * NODES * D_OUT)
@@ -71,13 +70,10 @@ def tile_graphattentionlayer_b_kernel(tc, h, W, a1, ef, a3, offs, out):
                 nc.sync.dma_start(offsets[:], offs)
             nc.sync.dma_start(a3_sb[t][:], a3[t * CHUNK:(t + 1) * CHUNK, :].rearrange("(b p) s -> p b s", p=P))
 
-        zeros = held.tile([P, CHUNK], BF16, name="zeros")
-        nc.vector.memset(zeros[:], 0.0)
-        idle_ps = flips.tile([P, CHUNK], F32, name="flip")
-        for i in range(WARM_UP):
-            nc.tensor.matmul(idle_ps[:], zeros[:, 0:P], zeros[:], start=True, stop=True)
+        zero = held.tile([P, 1], F32, name="zero")
+        nc.vector.memset(zero[:], 0.0)
         one = held.tile([P, 1], F32, name="one")
-        nc.scalar.activation(one[:], zeros[:, 0:1], EXP)
+        nc.scalar.activation(one[:], zero[:], EXP)
 
         identity = held.tile([P, P], F32, name="identity")
         make_identity(nc, identity[:])

from contextlib import ExitStack

import concourse.mybir as mybir
from concourse.masks import make_identity

F32 = mybir.dt.float32
BF16 = mybir.dt.bfloat16
U16 = mybir.dt.uint16
ADD = mybir.AluOpType.add
MAX = mybir.AluOpType.max
MIN = mybir.AluOpType.min
MULT = mybir.AluOpType.mult
EXP = mybir.ActivationFunctionType.Exp
IDENTITY = mybir.ActivationFunctionType.Identity

P = 128
D_IN, D_OUT, D_EDGE = 512, 512, 256
NODES, EDGES, DEGREE = 256, 8192, 32
ALPHA = 0.2
NEG_BIG = -9e15

K_IN, K_OUT, K_EDGE = D_IN // P, D_OUT // P, D_EDGE // P
BLOCKS = NODES // P
CHUNK = 512
PIECE = 256
CHUNKS = EDGES // CHUNK
PIECES = CHUNK // PIECE
HALF_PIECE = PIECE // 2
CUTS = ([(first, PIECE) for first in range(0, EDGES - PIECE, PIECE)]
        + [(first, HALF_PIECE) for first in range(EDGES - PIECE, EDGES, HALF_PIECE)])
STEPS = len(CUTS)
FLIP_LAG = 1
MIX_LAG = 3
VECTOR_SHARE = 4
HALF_IN = K_IN // 2

FLOPS = 2 * (D_IN * D_OUT * NODES + 2 * D_OUT * NODES * NODES + D_EDGE * NODES * EDGES
             + EDGES * NODES * NODES + NODES * NODES * D_OUT)


def tile_graphattentionlayer_b_kernel(tc, h, W, a1, ef, a3, offs, out):
    nc = tc.nc
    with ExitStack() as pools:
        held = pools.enter_context(tc.tile_pool(name="held", bufs=1))
        sums = pools.enter_context(tc.tile_pool(name="sums", bufs=8))
        picked = pools.enter_context(tc.tile_pool(name="picked", bufs=16))
        flipped = pools.enter_context(tc.tile_pool(name="flipped", bufs=8))
        tail = pools.enter_context(tc.tile_pool(name="tail", bufs=2))
        banks = pools.enter_context(tc.psum_pool(name="banks", bufs=4))
        flips = pools.enter_context(tc.psum_pool(name="flips", bufs=3))
        scores = pools.enter_context(tc.psum_pool(name="scores", bufs=1))

        h_f32 = [held.tile([P, HALF_IN, NODES], F32, name=f"h_f32_{i}") for i in range(2)]
        w_sb = [held.tile([P, HALF_IN, D_OUT], BF16, name=f"w_{i}") for i in range(2)]
        for i in range(2):
            rows = slice(i * HALF_IN * P, (i + 1) * HALF_IN * P)
            nc.sync.dma_start(h_f32[i][:], h[rows, :].rearrange("(k p) s -> p k s", p=P))
            nc.scalar.dma_start(w_sb[i][:], W[rows, :].rearrange("(k p) d -> p k d", p=P))
        a1_edges = held.tile([P, K_EDGE, NODES], BF16, name="a1_edges")
        nc.scalar.dma_start(a1_edges[:], a1[2 * D_OUT:2 * D_OUT + D_EDGE, :].rearrange("(k p) c -> p k c", p=P))
        a1_nodes = held.tile([P, 2 * K_OUT, NODES], BF16, name="a1_nodes")
        nc.scalar.dma_start(a1_nodes[:], a1[0:2 * D_OUT, :].rearrange("(k p) c -> p k c", p=P))
        offsets = held.tile([P, EDGES // 16], U16, name="offsets")
        ef_sb = [[held.tile([P, CHUNK], BF16, name=f"ef_{k}_{t}") for t in range(CHUNKS)] for k in range(K_EDGE)]
        a3_sb = [held.tile([P, CHUNK // P, NODES], BF16, name=f"a3_{t}") for t in range(CHUNKS)]
        for t in range(CHUNKS):
            for k in range(K_EDGE):
                nc.sync.dma_start(ef_sb[k][t][:], ef[k * P:(k + 1) * P, t * CHUNK:(t + 1) * CHUNK])
            if t == 0:
                nc.sync.dma_start(offsets[:], offs)
            nc.sync.dma_start(a3_sb[t][:], a3[t * CHUNK:(t + 1) * CHUNK, :].rearrange("(b p) s -> p b s", p=P))

        zero = held.tile([P, 1], F32, name="zero")
        nc.vector.memset(zero[:], 0.0)
        one = held.tile([P, 1], F32, name="one")
        nc.scalar.activation(one[:], zero[:], EXP)

        identity = held.tile([P, P], F32, name="identity")
        make_identity(nc, identity[:])

        identity_bf = held.tile([P, P], BF16, name="identity_bf")
        nc.vector.tensor_copy(identity_bf[:], identity[:])
        self_mask = held.tile([P, BLOCKS, NODES], BF16, name="self_mask")
        nc.vector.memset(self_mask[:], 0.0)
        for pb in range(BLOCKS):
            nc.vector.tensor_scalar_mul(self_mask[:, pb, pb * P:(pb + 1) * P], identity[:], NEG_BIG)

        def project_edges(t, c):
            bank = banks.tile([P, CHUNK], F32, name="bank")
            for k in range(K_EDGE):
                nc.tensor.matmul(bank[:], a1_edges[:, k, c * P:(c + 1) * P], ef_sb[k][t][:],
                                 start=(k == 0), stop=(k == K_EDGE - 1))
            return bank

        r_ps = [[None] * BLOCKS for t in range(CHUNKS)]

        h_bf = [held.tile([P, HALF_IN, NODES], BF16, name=f"h_bf_{i}") for i in range(2)]
        wh_ps = [(flips if d < K_OUT // 2 else banks).tile([P, NODES], F32, name="flip" if d < K_OUT // 2 else "bank")
                 for d in range(K_OUT)]
        for i in range(2):
            nc.vector.tensor_copy(h_bf[i][:], h_f32[i][:])
            for d in range(K_OUT):
                for k in range(HALF_IN):
                    nc.tensor.matmul(wh_ps[d][:], w_sb[i][:, k, d * P:(d + 1) * P], h_bf[i][:, k, :],
                                     start=(i == 0 and k == 0), stop=(i == 1 and k == HALF_IN - 1))
        r_ps[0][0] = project_edges(0, 0)
        wh_bf = held.tile([P, K_OUT, NODES], BF16, name="wh_bf")
        for d in range(K_OUT):
            if d % 2 == 0:
                nc.vector.tensor_copy(wh_bf[:, d, :], wh_ps[d][:])
            else:
                nc.scalar.copy(wh_bf[:, d, :], wh_ps[d][:])

        def project_nodes(first_row, c, pool, tag):
            product = pool.tile([P, NODES], F32, name=tag)
            for k in range(K_OUT):
                nc.tensor.matmul(product[:], a1_nodes[:, first_row + k, c * P:(c + 1) * P], wh_bf[:, k, :],
                                 start=(k == 0), stop=(k == K_OUT - 1))
            return product

        per_chunk = CHUNK // DEGREE
        per_piece = PIECE // DEGREE

        def add_targets_on_vector(t, c, first, end):
            edges = slice(first * DEGREE, end * DEGREE)
            nodes = slice(t * per_chunk + first, t * per_chunk + end)
            nc.vector.tensor_tensor(
                qr_sb[t][c][:, edges].rearrange("p (s e) -> p s e", e=DEGREE),
                r_ps[t][c][:, edges].rearrange("p (s e) -> p s e", e=DEGREE),
                q_sb[c][:, nodes].unsqueeze(2).to_broadcast([P, end - first, DEGREE]),
                ADD)

        def add_targets_on_scalar(t, c, first, end):
            for s in range(first, end):
                node = t * per_chunk + s
                nc.scalar.activation(qr_sb[t][c][:, s * DEGREE:(s + 1) * DEGREE], r_ps[t][c][:, s * DEGREE:(s + 1) * DEGREE],
                                     IDENTITY, bias=q_sb[c][:, node:node + 1])

        def look_up(u, c):
            first, edges = CUTS[u]
            column = first // 16
            t, start = divmod(first, CHUNK)
            nee = picked.tile([P, edges], F32, name="nee")
            nc.vector.tensor_tensor(nee[:], p_sb[c][:].indirect(offsets[:, column:column + edges // 16]),
                                    qr_sb[t][c][:, start:start + edges], ADD)
            return nee

        def flip(u, nee_sb, pool, tag, copy):
            edge_blocks = CUTS[u][1] // P
            flip_ps = pool.tile([P, edge_blocks, NODES], F32, name=tag)
            for b in range(edge_blocks):
                for c in range(BLOCKS):
                    nc.tensor.transpose(flip_ps[:, b, c * P:(c + 1) * P], nee_sb[c][:, b * P:(b + 1) * P], identity[:])
            turned = flipped.tile([P, edge_blocks, NODES], BF16, name="turned")
            copy(turned[:], flip_ps[:])
            return turned

        def mix(u, turned):
            first, edges = CUTS[u]
            for b in range(edges // P):
                j = first // P + b
                for pb in range(BLOCKS):
                    nc.tensor.matmul(e_ps[:, pb, :], a3_sb[j * P // CHUNK][:, j % (CHUNK // P), pb * P:(pb + 1) * P],
                                     turned[:, b, :], start=False, stop=(j == EDGES // P - 1 and pb == BLOCKS - 1))

        wh_t_bf = held.tile([P, BLOCKS, D_OUT], BF16, name="wh_t_bf")

        def project_nodes_turned(s):
            wh_t_ps = banks.tile([P, D_OUT], F32, name="bank")
            for i in range(2):
                for k in range(HALF_IN):
                    nc.tensor.matmul(wh_t_ps[:], h_bf[i][:, k, s * P:(s + 1) * P], w_sb[i][:, k, :],
                                     start=(i == 0 and k == 0), stop=(i == 1 and k == HALF_IN - 1))
            nc.scalar.copy(wh_t_bf[:, s, :], wh_t_ps[:])

        def open_scores():
            bank = scores.tile([P, BLOCKS, NODES], F32, name="score")
            nc.tensor.matmul(bank[:], identity_bf[:], self_mask[:], start=True, stop=False)
            return bank

        qr_sb = [[None] * BLOCKS for t in range(CHUNKS)]
        nee_sb = [[None] * BLOCKS for u in range(STEPS)]
        nee_t = [None] * STEPS

        q_sb = [held.tile([P, NODES], F32, name=f"q_{c}") for c in range(BLOCKS)]
        p_sb = [held.tile([P, NODES], F32, name=f"p_{c}") for c in range(BLOCKS)]
        nc.vector.tensor_copy(q_sb[0][:], project_nodes(K_OUT, 0, scores, "score")[:])
        nc.scalar.copy(p_sb[0][:], project_nodes(0, 0, flips, "flip")[:])
        qr_sb[0] = [sums.tile([P, CHUNK], F32, name="qr") for c in range(BLOCKS)]
        for piece in range(PIECES):
            add_targets_on_vector(0, 0, piece * per_piece, (piece + 1) * per_piece)
        nee_sb[0][0] = look_up(0, 0)
        r_ps[0][1] = project_edges(0, 1)
        nc.scalar.copy(q_sb[1][:], project_nodes(K_OUT, 1, flips, "flip")[:])
        add_targets_on_scalar(0, 1, 0, per_chunk)
        p_ps = project_nodes(0, 1, flips, "flip")
        for c in range(BLOCKS):
            r_ps[1][c] = project_edges(1, c)
        nc.vector.tensor_copy(p_sb[1][:], p_ps[:])
        nee_sb[1][0] = look_up(1, 0)
        for u in range(PIECES):
            nee_sb[u][1] = look_up(u, 1)

        for u in range(STEPS):
            t, piece = divmod(u, PIECES)
            if t > 0:
                nee_sb[u] = [look_up(u, c) for c in range(BLOCKS)]
            if t + 1 < CHUNKS:
                if piece == 0:
                    qr_sb[t + 1] = [sums.tile([P, CHUNK], F32, name="qr") for c in range(BLOCKS)]
                for c, by_scalar in ((0, per_chunk - VECTOR_SHARE), (1, per_chunk)):
                    add_targets_on_scalar(t + 1, c, piece * per_piece, min((piece + 1) * per_piece, by_scalar))
                if piece == PIECES - 1:
                    add_targets_on_vector(t + 1, 0, per_chunk - VECTOR_SHARE, per_chunk)
            if t + 2 < CHUNKS:
                r_ps[t + 2][piece] = project_edges(t + 2, piece)
            if u >= FLIP_LAG:
                copy = nc.scalar.copy if u < STEPS - 1 else nc.vector.tensor_copy
                nee_t[u - FLIP_LAG] = flip(u - FLIP_LAG, nee_sb[u - FLIP_LAG], flips, "flip", copy)
            if u == MIX_LAG:
                e_ps = open_scores()
            if u >= MIX_LAG:
                mix(u - MIX_LAG, nee_t[u - MIX_LAG])

        nee_t[STEPS - 1] = flip(STEPS - 1, nee_sb[STEPS - 1], banks, "bank", nc.scalar.copy)
        for u in range(STEPS - MIX_LAG, STEPS):
            mix(u, nee_t[u])

        weight = [tail.tile([P, NODES], F32, name="weight") for pb in range(BLOCKS)]
        total = [tail.tile([P, 1], F32, name="total") for pb in range(BLOCKS)]
        neg_scaled = [tail.tile([P, NODES], F32, name="neg_scaled") for pb in range(BLOCKS)]
        neg_peak = [tail.tile([P, 1], F32, name="neg_peak") for pb in range(BLOCKS)]
        neg_top = [tail.tile([P, 1], F32, name="neg_top") for pb in range(BLOCKS)]
        score = [tail.tile([P, NODES], F32, name="score") for pb in range(BLOCKS)]
        for pb in range(BLOCKS):
            nc.vector.tensor_scalar(neg_scaled[pb][:], e_ps[:, pb, :], -ALPHA, None, MULT, MIN, accum_out=neg_peak[pb][:])
        for pb in range(BLOCKS):
            nc.vector.scalar_tensor_tensor(neg_top[pb][:], neg_peak[pb][:], 1.0 / ALPHA, neg_peak[pb][:], MULT, MIN)
            nc.vector.scalar_tensor_tensor(score[pb][:], neg_scaled[pb][:], -1.0, e_ps[:, pb, :], MULT, MAX)
            nc.scalar.activation(weight[pb][:], score[pb][:], EXP, bias=neg_top[pb][:], accum_out=total[pb][:])

        for s in range(BLOCKS):
            project_nodes_turned(s)

        att_t_ps = [flips.tile([P, BLOCKS, P], BF16, name="flip") for pb in range(BLOCKS)]
        for pb in range(BLOCKS):
            inverse = tail.tile([P, 1], F32, name="inverse")
            nc.vector.reciprocal(inverse[:], total[pb][:])
            att = tail.tile([P, NODES], BF16, name="att")
            nc.vector.tensor_scalar_mul(att[:], weight[pb][:], inverse[:])
            for c in range(BLOCKS):
                nc.tensor.transpose(att_t_ps[pb][:, c, :], att[:, c * P:(c + 1) * P], identity_bf[:])
        att_t_bf = [tail.tile([P, BLOCKS, P], BF16, name="att_t_bf") for pb in range(BLOCKS)]
        for pb in range(BLOCKS):
            nc.vector.tensor_copy(att_t_bf[pb][:], att_t_ps[pb][:])

        HALF = K_OUT // 2
        out_ps = [[banks.tile([P, HALF, P], F32, name="bank") for half in range(2)] for pb in range(BLOCKS)]
        for pb in range(BLOCKS):
            for d in range(K_OUT):
                for c in range(BLOCKS):
                    nc.tensor.matmul(out_ps[pb][d // HALF][:, d % HALF, :], wh_t_bf[:, c, d * P:(d + 1) * P],
                                     att_t_bf[pb][:, c, :], start=(c == 0), stop=(c == BLOCKS - 1))
        out_blocks = out.rearrange("(k p) s -> p k s", p=P)
        for pb in range(BLOCKS):
            out_sb = tail.tile([P, K_OUT, P], F32, name="out_sb")
            nc.scalar.copy(out_sb[:, 0:HALF, :], out_ps[pb][0][:])
            nc.vector.tensor_copy(out_sb[:, HALF:K_OUT, :], out_ps[pb][1][:])
            nc.scalar.dma_start(out_blocks[:, 0:HALF, pb * P:(pb + 1) * P], out_sb[:, 0:HALF, :])
            nc.sync.dma_start(out_blocks[:, HALF:K_OUT, pb * P:(pb + 1) * P], out_sb[:, HALF:K_OUT, :])
